import numpy as np
import ml_dtypes


def mxq(x, axis, fmt="e4m3"):
    dtype, down = {"e4m3": (ml_dtypes.float8_e4m3fn, 7), "e5m2": (ml_dtypes.float8_e5m2, 14)}[fmt]
    v = np.moveaxis(np.asarray(x, np.float32).astype(ml_dtypes.bfloat16).astype(np.float64), axis, -1)
    blocks = v.reshape(v.shape[:-1] + (-1, 32))
    amax = np.abs(blocks).max(-1, keepdims=True)
    byte = np.maximum(np.where(amax > 0, np.frexp(amax)[1] - 1 + 127, 0) - down, 1)
    scale = np.exp2(byte - 127.0)
    codes = (blocks / scale).astype(np.float32).astype(dtype).astype(np.float64)
    return np.moveaxis((codes * scale).reshape(v.shape), -1, axis)


WIDE = False


def mx_kscale(k):
    if not WIDE:
        return np.ones(k)
    levels = np.array([10, -10, 5, -5, 0])
    a = np.random.permutation(np.resize(levels, k // 512 * 4)).reshape(k // 512, 4)
    idx = np.arange(k)
    return np.exp2(a[idx // 512, idx % 128 // 32])


BF16 = ml_dtypes.bfloat16


def bf(x):
    return np.asarray(x, np.float32).astype(BF16)


def f64(x):
    return np.asarray(x).astype(np.float64)


B, C, H, W = 28, 512, 16, 16
N = H * W
EPS = 1e-5
XS = np.sqrt((np.log(C) + 2.0) / N)


def setup_inputs():
    s = mx_kscale(C)
    s = s / s.max()
    return {"x": bf(np.random.standard_normal((B, C, H, W)) * XS * s[None, :, None, None]),
            "conv_w": bf(np.random.standard_normal((C, C)) / (XS * np.sqrt(C)) / s[None, :]),
            "gamma": bf(1.0 + 0.1 * np.random.standard_normal(C)),
            "beta": bf(0.1 * np.random.standard_normal(C))}


def reference(x, conv_w, gamma, beta):
    x, conv_w, gamma, beta = f64(x), f64(conv_w), f64(gamma), f64(beta)
    b, c, h, w = x.shape
    xr = x.reshape(b, c, h * w)
    xq = mxq(xr, 1, "e4m3")
    y = mxq(conv_w, 1, "e4m3") @ xq
    mean = y.mean(axis=(0, 2))
    var = (y ** 2).mean(axis=(0, 2)) - mean ** 2
    inv = gamma / np.sqrt(var + EPS)
    y = np.maximum(y * inv[None, :, None] + (beta - mean * inv)[None, :, None], 0.0)
    g = xr @ xr.transpose(0, 2, 1)
    e = np.exp(g - g.max(-1, keepdims=True))
    att = e / e.sum(-1, keepdims=True)
    sp = mxq(att, 2, "e4m3") @ xq
    return (y + sp).reshape(b, c, h, w)

@@ -1,0 +1,244 @@
+from contextlib import ExitStack
+
+import concourse.mybir as mybir
+from concourse.masks import make_identity
+
+F32 = mybir.dt.float32
+BF16 = mybir.dt.bfloat16
+U32 = mybir.dt.uint32
+U8 = mybir.dt.uint8
+FP8X4 = mybir.dt.float8_e4m3fn_x4
+ACT = mybir.ActivationFunctionType
+ALU = mybir.AluOpType
+AX = mybir.AxisListType
+
+B = 28
+C = 512
+N = 256
+P = 128
+T = 4
+EPS = 1e-5
+PAIRS = B // 2
+FLOPS = 3 * 2 * B * C * C * N
+
+
+def tile_informationinteraction_t_kernel(tc, x, conv_w, gamma, beta, out):
+    nc = tc.nc
+    x_v = x.rearrange("b (p t) h w -> p b (t h w)", t=T)
+    out_v = out.rearrange("b (m a) h w -> m b (a h w)", a=T)
+    w_v = conv_w.rearrange("(m a) c -> m (a c)", a=T)
+
+    with ExitStack() as ctx:
+        keep = ctx.enter_context(tc.tile_pool(name="keep", bufs=1))
+
+        ident = keep.tile([P, P], BF16)
+        make_identity(nc, ident[:])
+
+        xq = keep.tile([P, B * N], U32, align_bytes=64)
+        xs = keep.tile([P, B * N], U8, align_bytes=64)
+        aq = keep.tile([P, B * C], U32, align_bytes=64)
+        asc = keep.tile([P, B * C], U8, align_bytes=64)
+        wq = keep.tile([P, C], U32, align_bytes=64)
+        ws = keep.tile([P, C], U8, align_bytes=64)
+        st = keep.tile([P, T, PAIRS, 6], F32)
+        inv = keep.tile([P, T], F32)
+        shift = keep.tile([P, T], F32)
+        gam_b = keep.tile([P, T], BF16)
+        bet_b = keep.tile([P, T], BF16)
+
+        with ExitStack() as pa:
+            xpool = pa.enter_context(tc.tile_pool(name="xpool", bufs=1))
+            work = pa.enter_context(tc.tile_pool(name="work", bufs=2))
+            epool = pa.enter_context(tc.tile_pool(name="epool", bufs=8))
+            small = pa.enter_context(tc.tile_pool(name="small", bufs=4))
+            ps_g = pa.enter_context(tc.psum_pool(name="ps_g", bufs=4))
+            ps_t = pa.enter_context(tc.psum_pool(name="ps_t", bufs=2))
+            ps_x = pa.enter_context(tc.psum_pool(name="ps_x", bufs=1))
+            ps_y = pa.enter_context(tc.psum_pool(name="ps_y", bufs=1))
+
+            x_sb = xpool.tile([P, B, T, N], BF16)
+            w_sb = xpool.tile([P, T, C], BF16)
+            x_flat = x_sb[:].rearrange("p b t n -> p b (t n)")
+            nc.sync.dma_start(out=x_flat[:, 0:1, :], in_=x_v[:, 0:1, :])
+            nc.sync.dma_start(out=x_flat[:, 1:4, :], in_=x_v[:, 1:4, :])
+            nc.sync.dma_start(out=w_sb[:].rearrange("m a c -> m (a c)"), in_=w_v)
+            for b0 in range(4, B, 4):
+                nc.sync.dma_start(out=x_flat[:, b0:b0 + 4, :], in_=x_v[:, b0:b0 + 4, :])
+            nc.scalar.dma_start(out=gam_b[:], in_=gamma.rearrange("(m a) -> m a", a=T))
+            nc.scalar.dma_start(out=bet_b[:], in_=beta.rearrange("(m a) -> m a", a=T))
+
+            w_perm = xpool.tile([P, T, T, P], BF16)
+            nc.vector.tensor_copy(
+                out=w_perm[:], in_=w_sb[:].rearrange("m a (p t) -> m a t p", t=T)
+            )
+            w_grp = xpool.tile([P, T, P, T], BF16, align_bytes=64)
+            for a0 in range(0, T, 2):
+                wt = ps_t.tile([P, 2, T, P], BF16, tag="pt")
+                for a2 in range(2):
+                    for t in range(T):
+                        nc.tensor.transpose(
+                            out=wt[:, a2, t, :], in_=w_perm[:, a0 + a2, t, :], identity=ident[:]
+                        )
+                nc.vector.tensor_copy(
+                    out=w_grp[:, a0:a0 + 2, :, :], in_=wt[:].rearrange("p a t m -> p a m t")
+                )
+            nc.vector.quantize_mx(
+                out=wq[:].bitcast(FP8X4),
+                scales=ws[:],
+                in_=w_grp[:].rearrange("p a m t -> p (a m t)"),
+            )
+
+            for q in range(PAIRS):
+                xg = work.tile([P, 2, N, T], BF16, align_bytes=64)
+                for j in range(2):
+                    nc.vector.tensor_copy(
+                        out=xg[:, j].rearrange("p (c i) t -> p c t i", i=4),
+                        in_=x_sb[:, 2 * q + j].rearrange("p t (c i) -> p c t i", i=4),
+                    )
+                cols = slice(q * 2 * N, (q + 1) * 2 * N)
+                nc.vector.quantize_mx(
+                    out=xq[:, cols].bitcast(FP8X4),
+                    scales=xs[:, cols],
+                    in_=xg[:].rearrange("p j n t -> p (j n t)"),
+                )
+                for a in range(T):
+                    y_ps = ps_y.tile([P, 2 * N], F32)
+                    nc.tensor.matmul_mx(
+                        out=y_ps[:],
+                        lhsT=wq[:, a * P:(a + 1) * P].bitcast(FP8X4),
+                        lhsT_scale=ws[:, a * P:(a + 1) * P],
+                        rhs=xq[:, cols].bitcast(FP8X4),
+                        rhs_scale=xs[:, cols],
+                        start=True,
+                        stop=True,
+                    )
+                    nc.vector.bn_stats(out=st[:, a, q, :], in_=y_ps[:])
+
+                for b in (2 * q, 2 * q + 1):
+                    xt_ps = ps_x.tile([P, 2, C], BF16)
+                    for h in range(2):
+                        for t in range(T):
+                            nc.tensor.transpose(
+                                out=xt_ps[:, h, t * P:(t + 1) * P],
+                                in_=x_sb[:, b, t, h * P:(h + 1) * P],
+                                identity=ident[:],
+                            )
+                    xT = work.tile([P, 2, C], BF16)
+                    nc.scalar.copy(out=xT[:], in_=xt_ps[:])
+
+                    nm = small.tile([P, T], F32)
+                    ssum = small.tile([P, T], F32)
+                    rs = small.tile([P, T], F32)
+                    es = []
+                    for a in range(T):
+                        g_ps = ps_g.tile([P, C], F32)
+                        for h in range(2):
+                            nc.tensor.matmul(
+                                out=g_ps[:],
+                                lhsT=xT[:, h, a * P:(a + 1) * P],
+                                rhs=xT[:, h, :],
+                                start=(h == 0),
+                                stop=(h == 1),
+                            )
+                        nc.vector.tensor_reduce(
+                            out=nm[:, a:a + 1], in_=g_ps[:], axis=AX.X, op=ALU.max, negate=True
+                        )
+                        e = epool.tile([P, C], F32)
+                        nc.scalar.activation(
+                            out=e[:],
+                            in_=g_ps[:],
+                            func=ACT.Exp,
+                            bias=nm[:, a:a + 1],
+                            scale=1.0,
+                            accum_out=ssum[:, a:a + 1],
+                        )
+                        es.append(e)
+                    nc.vector.reciprocal(out=rs[:], in_=ssum[:])
+                    ag = work.tile([P, T, P, T], BF16, align_bytes=64)
+                    for a0 in range(0, T, 2):
+                        pt = ps_t.tile([P, 2, T, P], BF16, tag="pt")
+                        for a2 in range(2):
+                            a = a0 + a2
+                            att = epool.tile([P, C], BF16)
+                            nc.gpsimd.tensor_scalar(
+                                out=att[:],
+                                in0=es[a][:],
+                                scalar1=rs[:, a:a + 1],
+                                scalar2=0.0,
+                                op0=ALU.mult,
+                                op1=ALU.add,
+                            )
+                            for t in range(T):
+                                nc.tensor.transpose(
+                                    out=pt[:, a2, t, :],
+                                    in_=att[:, t * P:(t + 1) * P],
+                                    identity=ident[:],
+                                )
+                        nc.scalar.copy(
+                            out=ag[:, a0:a0 + 2, :, :], in_=pt[:].rearrange("p a t m -> p a m t")
+                        )
+                    nc.vector.quantize_mx(
+                        out=aq[:, b * C:(b + 1) * C].bitcast(FP8X4),
+                        scales=asc[:, b * C:(b + 1) * C],
+                        in_=ag[:].rearrange("p a m t -> p (a m t)"),
+                    )
+
+            mv = small.tile([P, T, 2], F32)
+            for a in range(T):
+                nc.vector.bn_aggr(out=mv[:, a, :], in_=st[:, a].rearrange("p q s -> p (q s)"))
+            gam = small.tile([P, T], F32)
+            bet = small.tile([P, T], F32)
+            nc.vector.tensor_copy(out=gam[:], in_=gam_b[:])
+            nc.vector.tensor_copy(out=bet[:], in_=bet_b[:])
+            sd = small.tile([P, T], F32)
+            nc.vector.tensor_scalar_add(out=sd[:], in0=mv[:, :, 1], scalar1=EPS)
+            nc.scalar.sqrt(out=sd[:], in_=sd[:])
+            nc.vector.reciprocal(out=sd[:], in_=sd[:])
+            nc.vector.tensor_mul(out=inv[:], in0=gam[:], in1=sd[:])
+            mi = small.tile([P, T], F32)
+            nc.vector.tensor_mul(out=mi[:], in0=mv[:, :, 0], in1=inv[:])
+            nc.vector.tensor_sub(out=shift[:], in0=bet[:], in1=mi[:])
+
+        with ExitStack() as pb:
+            rpool = pb.enter_context(tc.tile_pool(name="rpool", bufs=4))
+            opool = pb.enter_context(tc.tile_pool(name="opool", bufs=3))
+            ps_c = pb.enter_context(tc.psum_pool(name="ps_c", bufs=4))
+            ps_s = pb.enter_context(tc.psum_pool(name="ps_s", bufs=4))
+            for q in range(PAIRS):
+                cols = slice(q * 2 * N, (q + 1) * 2 * N)
+                o_sb = opool.tile([P, 2, T, N], F32)
+                for a in range(T):
+                    y2 = ps_c.tile([P, 2 * N], F32)
+                    nc.tensor.matmul_mx(
+                        out=y2[:],
+                        lhsT=wq[:, a * P:(a + 1) * P].bitcast(FP8X4),
+                        lhsT_scale=ws[:, a * P:(a + 1) * P],
+                        rhs=xq[:, cols].bitcast(FP8X4),
+                        rhs_scale=xs[:, cols],
+                        start=True,
+                        stop=True,
+                    )
+                    sp = ps_s.tile([P, 2, N], F32)
+                    for j in range(2):
+                        b = 2 * q + j
+                        nc.tensor.matmul_mx(
+                            out=sp[:, j, :],
+                            lhsT=aq[:, b * C + a * P:b * C + (a + 1) * P].bitcast(FP8X4),
+                            lhsT_scale=asc[:, b * C + a * P:b * C + (a + 1) * P],
+                            rhs=xq[:, b * N:(b + 1) * N].bitcast(FP8X4),
+                            rhs_scale=xs[:, b * N:(b + 1) * N],
+                            start=True,
+                            stop=True,
+                        )
+                    r = rpool.tile([P, 2, N], F32)
+                    nc.scalar.activation(
+                        out=r[:].rearrange("p j n -> p (j n)"),
+                        in_=y2[:],
+                        func=ACT.Relu,
+                        bias=shift[:, a:a + 1],
+                        scale=inv[:, a:a + 1],
+                    )
+                    nc.vector.tensor_tensor(out=o_sb[:, :, a, :], in0=sp[:], in1=r[:], op=ALU.add)
+                nc.sync.dma_start(
+                    out=out_v[:, 2 * q:2 * q + 2, :], in_=o_sb[:].rearrange("p j a n -> p j (a n)")
+                )

@@ -19,6 +19,8 @@ P = 128
 T = 4
 EPS = 1e-5
 PAIRS = B // 2
+UNITS = PAIRS * T
+GROUP = 4
 FLOPS = 3 * 2 * B * C * C * N
 
 
@@ -30,215 +32,334 @@ def tile_informationinteraction_t_kernel(tc, x, conv_w, gamma, beta, out):
 
     with ExitStack() as ctx:
         keep = ctx.enter_context(tc.tile_pool(name="keep", bufs=1))
+        big = ctx.enter_context(tc.tile_pool(name="big", bufs=5))
+        work = ctx.enter_context(tc.tile_pool(name="work", bufs=2))
+        epool = ctx.enter_context(tc.tile_pool(name="epool", bufs=8))
+        small = ctx.enter_context(tc.tile_pool(name="small", bufs=4))
+        ps_g = ctx.enter_context(tc.psum_pool(name="ps_g", bufs=4))
+        ps_t = ctx.enter_context(tc.psum_pool(name="ps_t", bufs=2))
+        ps_x = ctx.enter_context(tc.psum_pool(name="ps_x", bufs=1))
+        ps_y = ctx.enter_context(tc.psum_pool(name="ps_y", bufs=1))
+        ctx.enter_context(tc.manual_schedule())
 
-        ident = keep.tile([P, P], BF16)
-        make_identity(nc, ident[:])
+        ident = keep.tile([P, P], BF16, name="ident")
+        ident32 = keep.tile([P, P], F32, name="ident32")
+        mhalf = keep.tile([P, T], F32, name="mhalf")
+        xq = keep.tile([P, B * N], U32, name="xq", align_bytes=64)
+        xs = keep.tile([P, B * N], U8, name="xs", align_bytes=64)
+        aq = keep.tile([P, B * C], U32, name="aq", align_bytes=64)
+        asc = keep.tile([P, B * C], U8, name="asc", align_bytes=64)
+        wq = keep.tile([P, C], U32, name="wq", align_bytes=64)
+        ws = keep.tile([P, C], U8, name="ws", align_bytes=64)
+        st = keep.tile([P, T, PAIRS, 6], F32, name="st")
+        mv = keep.tile([P, T, 2], F32, name="mv")
+        inv = keep.tile([P, T], F32, name="inv")
+        shift = keep.tile([P, T], F32, name="shift")
+        gam_b = keep.tile([P, T], BF16, name="gam_b")
+        bet_b = keep.tile([P, T], BF16, name="bet_b")
+        gam = keep.tile([P, T], F32, name="gam")
+        bet = keep.tile([P, T], F32, name="bet")
+        ve = keep.tile([P, T], F32, name="ve")
+        rsd = keep.tile([P, T], F32, name="rsd")
+        mi = keep.tile([P, T], F32, name="mi")
+        w_sb = keep.tile([P, T, C], BF16, name="w_sb")
+        w_grp = keep.tile([P, T, P, T], BF16, name="w_grp", align_bytes=64)
 
-        xq = keep.tile([P, B * N], U32, align_bytes=64)
-        xs = keep.tile([P, B * N], U8, align_bytes=64)
-        aq = keep.tile([P, B * C], U32, align_bytes=64)
-        asc = keep.tile([P, B * C], U8, align_bytes=64)
-        wq = keep.tile([P, C], U32, align_bytes=64)
-        ws = keep.tile([P, C], U8, align_bytes=64)
-        st = keep.tile([P, T, PAIRS, 6], F32)
-        inv = keep.tile([P, T], F32)
-        shift = keep.tile([P, T], F32)
-        gam_b = keep.tile([P, T], BF16)
-        bet_b = keep.tile([P, T], BF16)
+        xgrp = {}
+        xt_ps = {}
+        xT = {}
+        g_ps = {}
+        nm = {}
+        ssum = {}
+        rs = {}
+        ex = {}
+        att = {}
+        pt = {}
+        ag = {}
+        xg = {}
+        y_ps = {}
 
-        with ExitStack() as pa:
-            xpool = pa.enter_context(tc.tile_pool(name="xpool", bufs=1))
-            work = pa.enter_context(tc.tile_pool(name="work", bufs=2))
-            epool = pa.enter_context(tc.tile_pool(name="epool", bufs=8))
-            small = pa.enter_context(tc.tile_pool(name="small", bufs=4))
-            ps_g = pa.enter_context(tc.psum_pool(name="ps_g", bufs=4))
-            ps_t = pa.enter_context(tc.psum_pool(name="ps_t", bufs=2))
-            ps_x = pa.enter_context(tc.psum_pool(name="ps_x", bufs=1))
-            ps_y = pa.enter_context(tc.psum_pool(name="ps_y", bufs=1))
+        def load_group(k, cuts):
+            xgrp[k] = big.tile([P, GROUP, T, N], BF16, name="xgrp", tag="big")
+            flat = xgrp[k][:].rearrange("p b t n -> p b (t n)")
+            for lo, hi in cuts:
+                nc.sync.dma_start(
+                    out=flat[:, lo:hi, :], in_=x_v[:, k * GROUP + lo:k * GROUP + hi, :]
+                )
 
-            x_sb = xpool.tile([P, B, T, N], BF16)
-            w_sb = xpool.tile([P, T, C], BF16)
-            x_flat = x_sb[:].rearrange("p b t n -> p b (t n)")
-            nc.sync.dma_start(out=x_flat[:, 0:1, :], in_=x_v[:, 0:1, :])
-            nc.sync.dma_start(out=x_flat[:, 1:4, :], in_=x_v[:, 1:4, :])
-            nc.sync.dma_start(out=w_sb[:].rearrange("m a c -> m (a c)"), in_=w_v)
-            for b0 in range(4, B, 4):
-                nc.sync.dma_start(out=x_flat[:, b0:b0 + 4, :], in_=x_v[:, b0:b0 + 4, :])
-            nc.scalar.dma_start(out=gam_b[:], in_=gamma.rearrange("(m a) -> m a", a=T))
-            nc.scalar.dma_start(out=bet_b[:], in_=beta.rearrange("(m a) -> m a", a=T))
+        def x_of(b):
+            return xgrp[b // GROUP][:, b % GROUP]
 
-            w_perm = xpool.tile([P, T, T, P], BF16)
-            nc.vector.tensor_copy(
-                out=w_perm[:], in_=w_sb[:].rearrange("m a (p t) -> m a t p", t=T)
+        def tx(b):
+            if not 0 <= b < B:
+                return
+            xt_ps[b] = ps_x.tile([P, 2, C], BF16, name="xt_ps", tag="x")
+            for h in range(2):
+                for t in range(T):
+                    nc.tensor.transpose(
+                        out=xt_ps[b][:, h, t * P:(t + 1) * P],
+                        in_=x_of(b)[:, t, h * P:(h + 1) * P],
+                        identity=ident[:],
+                    )
+
+        def xe(b):
+            if not 0 <= b < B:
+                return
+            xT[b] = work.tile([P, 2, C], BF16, name="xT", tag="xT")
+            nc.scalar.copy(out=xT[b][:], in_=xt_ps[b][:])
+
+        def gm(b, a):
+            if not 0 <= b < B:
+                return
+            g_ps[b, a] = ps_g.tile([P, C], F32, name="g_ps", tag="g")
+            for h in range(2):
+                nc.tensor.matmul(
+                    out=g_ps[b, a][:],
+                    lhsT=xT[b][:, h, a * P:(a + 1) * P],
+                    rhs=xT[b][:, h, :],
+                    start=(h == 0),
+                    stop=(h == 1),
+                )
+
+        def mx(b, a):
+            if not 0 <= b < B:
+                return
+            if a == 0:
+                nm[b] = small.tile([P, T], F32, name="nm", tag="nm")
+            nc.vector.tensor_reduce(
+                out=nm[b][:, a:a + 1], in_=g_ps[b, a][:], axis=AX.X, op=ALU.max, negate=True
             )
-            w_grp = xpool.tile([P, T, P, T], BF16, align_bytes=64)
-            for a0 in range(0, T, 2):
-                wt = ps_t.tile([P, 2, T, P], BF16, tag="pt")
+
+        def exq(b, a):
+            if not 0 <= b < B:
+                return
+            if a == 0:
+                ssum[b] = small.tile([P, T], F32, name="ssum", tag="ssum")
+            ex[b, a] = epool.tile([P, C], F32, name="ex", tag="e")
+            nc.scalar.activation(
+                out=ex[b, a][:],
+                in_=g_ps[b, a][:],
+                func=ACT.Exp,
+                bias=nm[b][:, a:a + 1],
+                scale=1.0,
+                accum_out=ssum[b][:, a:a + 1],
+            )
+
+        def rc(b):
+            if not 0 <= b < B:
+                return
+            rs[b] = small.tile([P, T], F32, name="rs", tag="rs")
+            nc.vector.reciprocal(out=rs[b][:], in_=ssum[b][:])
+
+        def nrm(b, a):
+            if not 0 <= b < B:
+                return
+            att[b, a] = epool.tile([P, C], BF16, name="att", tag="att")
+            nc.gpsimd.tensor_scalar(
+                out=att[b, a][:],
+                in0=ex[b, a][:],
+                scalar1=rs[b][:, a:a + 1],
+                scalar2=0.0,
+                op0=ALU.mult,
+                op1=ALU.add,
+            )
+
+        def ta(b, k):
+            if not 0 <= b < B:
+                return
+            pt[b, k] = ps_t.tile([P, 2, T, P], BF16, name="pt", tag="pt")
+            for a2 in range(2):
+                for t in range(T):
+                    nc.tensor.transpose(
+                        out=pt[b, k][:, a2, t, :],
+                        in_=att[b, 2 * k + a2][:, t * P:(t + 1) * P],
+                        identity=ident[:],
+                    )
+
+        def ae(b, k):
+            if not 0 <= b < B:
+                return
+            if k == 0:
+                ag[b] = work.tile([P, T, P, T], BF16, name="ag", tag="ag", align_bytes=64)
+            nc.scalar.copy(
+                out=ag[b][:, 2 * k:2 * k + 2, :, :],
+                in_=pt[b, k][:].rearrange("p a t m -> p a m t"),
+            )
+
+        def qa(b):
+            if not 0 <= b < B:
+                return
+            nc.vector.quantize_mx(
+                out=aq[:, b * C:(b + 1) * C].bitcast(FP8X4),
+                scales=asc[:, b * C:(b + 1) * C],
+                in_=ag[b][:].rearrange("p a m t -> p (a m t)"),
+            )
+
+        def xr(b):
+            if not 0 <= b < B:
+                return
+            if b % 2 == 0:
+                xg[b // 2] = work.tile([P, 2, N, T], BF16, name="xg", tag="xg", align_bytes=64)
+            nc.vector.tensor_copy(
+                out=xg[b // 2][:, b % 2].rearrange("p (c i) t -> p c t i", i=4),
+                in_=x_of(b).rearrange("p t (c i) -> p c t i", i=4),
+            )
+
+        def qx(q):
+            if not 0 <= q < PAIRS:
+                return
+            cols = slice(q * 2 * N, (q + 1) * 2 * N)
+            nc.vector.quantize_mx(
+                out=xq[:, cols].bitcast(FP8X4),
+                scales=xs[:, cols],
+                in_=xg[q][:].rearrange("p j n t -> p (j n t)"),
+            )
+
+        def conv(dst, q, a):
+            cols = slice(q * 2 * N, (q + 1) * 2 * N)
+            nc.tensor.matmul_mx(
+                out=dst,
+                lhsT=wq[:, a * P:(a + 1) * P].bitcast(FP8X4),
+                lhsT_scale=ws[:, a * P:(a + 1) * P],
+                rhs=xq[:, cols].bitcast(FP8X4),
+                rhs_scale=xs[:, cols],
+                start=True,
+                stop=True,
+            )
+
+        def cv(u):
+            if not 0 <= u < UNITS:
+                return
+            y_ps[u] = ps_y.tile([P, 2 * N], F32, name="y_ps", tag="y")
+            conv(y_ps[u][:], u // T, u % T)
+
+        def bs(u):
+            if not 0 <= u < UNITS:
+                return
+            nc.vector.bn_stats(out=st[:, u % T, u // T, :], in_=y_ps[u][:])
+
+        def w_transposes():
+            w32 = w_sb[:].bitcast(F32).rearrange("m a (p u) -> m a u p", u=2)
+            g32 = w_grp[:].rearrange("p a m t -> p a (m t)").bitcast(F32).rearrange(
+                "p a (m u) -> p a m u", u=2
+            )
+            for k in range(2):
+                wt = ps_t.tile([P, 2, 2, P], F32, name="wt", tag="pt")
                 for a2 in range(2):
-                    for t in range(T):
+                    for u in range(2):
                         nc.tensor.transpose(
-                            out=wt[:, a2, t, :], in_=w_perm[:, a0 + a2, t, :], identity=ident[:]
+                            out=wt[:, a2, u, :], in_=w32[:, 2 * k + a2, u, :], identity=ident32[:]
                         )
                 nc.vector.tensor_copy(
-                    out=w_grp[:, a0:a0 + 2, :, :], in_=wt[:].rearrange("p a t m -> p a m t")
+                    out=g32[:, 2 * k:2 * k + 2], in_=wt[:].rearrange("p a u m -> p a m u")
                 )
+
+        def w_quantise():
             nc.vector.quantize_mx(
                 out=wq[:].bitcast(FP8X4),
                 scales=ws[:],
                 in_=w_grp[:].rearrange("p a m t -> p (a m t)"),
             )
 
-            for q in range(PAIRS):
-                xg = work.tile([P, 2, N, T], BF16, align_bytes=64)
-                for j in range(2):
-                    nc.vector.tensor_copy(
-                        out=xg[:, j].rearrange("p (c i) t -> p c t i", i=4),
-                        in_=x_sb[:, 2 * q + j].rearrange("p t (c i) -> p c t i", i=4),
-                    )
-                cols = slice(q * 2 * N, (q + 1) * 2 * N)
-                nc.vector.quantize_mx(
-                    out=xq[:, cols].bitcast(FP8X4),
-                    scales=xs[:, cols],
-                    in_=xg[:].rearrange("p j n t -> p (j n t)"),
-                )
-                for a in range(T):
-                    y_ps = ps_y.tile([P, 2 * N], F32)
-                    nc.tensor.matmul_mx(
-                        out=y_ps[:],
-                        lhsT=wq[:, a * P:(a + 1) * P].bitcast(FP8X4),
-                        lhsT_scale=ws[:, a * P:(a + 1) * P],
-                        rhs=xq[:, cols].bitcast(FP8X4),
-                        rhs_scale=xs[:, cols],
-                        start=True,
-                        stop=True,
-                    )
-                    nc.vector.bn_stats(out=st[:, a, q, :], in_=y_ps[:])
-
-                for b in (2 * q, 2 * q + 1):
-                    xt_ps = ps_x.tile([P, 2, C], BF16)
-                    for h in range(2):
-                        for t in range(T):
-                            nc.tensor.transpose(
-                                out=xt_ps[:, h, t * P:(t + 1) * P],
-                                in_=x_sb[:, b, t, h * P:(h + 1) * P],
-                                identity=ident[:],
-                            )
-                    xT = work.tile([P, 2, C], BF16)
-                    nc.scalar.copy(out=xT[:], in_=xt_ps[:])
-
-                    nm = small.tile([P, T], F32)
-                    ssum = small.tile([P, T], F32)
-                    rs = small.tile([P, T], F32)
-                    es = []
-                    for a in range(T):
-                        g_ps = ps_g.tile([P, C], F32)
-                        for h in range(2):
-                            nc.tensor.matmul(
-                                out=g_ps[:],
-                                lhsT=xT[:, h, a * P:(a + 1) * P],
-                                rhs=xT[:, h, :],
-                                start=(h == 0),
-                                stop=(h == 1),
-                            )
-                        nc.vector.tensor_reduce(
-                            out=nm[:, a:a + 1], in_=g_ps[:], axis=AX.X, op=ALU.max, negate=True
-                        )
-                        e = epool.tile([P, C], F32)
-                        nc.scalar.activation(
-                            out=e[:],
-                            in_=g_ps[:],
-                            func=ACT.Exp,
-                            bias=nm[:, a:a + 1],
-                            scale=1.0,
-                            accum_out=ssum[:, a:a + 1],
-                        )
-                        es.append(e)
-                    nc.vector.reciprocal(out=rs[:], in_=ssum[:])
-                    ag = work.tile([P, T, P, T], BF16, align_bytes=64)
-                    for a0 in range(0, T, 2):
-                        pt = ps_t.tile([P, 2, T, P], BF16, tag="pt")
-                        for a2 in range(2):
-                            a = a0 + a2
-                            att = epool.tile([P, C], BF16)
-                            nc.gpsimd.tensor_scalar(
-                                out=att[:],
-                                in0=es[a][:],
-                                scalar1=rs[:, a:a + 1],
-                                scalar2=0.0,
-                                op0=ALU.mult,
-                                op1=ALU.add,
-                            )
-                            for t in range(T):
-                                nc.tensor.transpose(
-                                    out=pt[:, a2, t, :],
-                                    in_=att[:, t * P:(t + 1) * P],
-                                    identity=ident[:],
-                                )
-                        nc.scalar.copy(
-                            out=ag[:, a0:a0 + 2, :, :], in_=pt[:].rearrange("p a t m -> p a m t")
-                        )
-                    nc.vector.quantize_mx(
-                        out=aq[:, b * C:(b + 1) * C].bitcast(FP8X4),
-                        scales=asc[:, b * C:(b + 1) * C],
-                        in_=ag[:].rearrange("p a m t -> p (a m t)"),
-                    )
-
-            mv = small.tile([P, T, 2], F32)
+        def bn_constants():
             for a in range(T):
                 nc.vector.bn_aggr(out=mv[:, a, :], in_=st[:, a].rearrange("p q s -> p (q s)"))
-            gam = small.tile([P, T], F32)
-            bet = small.tile([P, T], F32)
-            nc.vector.tensor_copy(out=gam[:], in_=gam_b[:])
-            nc.vector.tensor_copy(out=bet[:], in_=bet_b[:])
-            sd = small.tile([P, T], F32)
-            nc.vector.tensor_scalar_add(out=sd[:], in0=mv[:, :, 1], scalar1=EPS)
-            nc.scalar.sqrt(out=sd[:], in_=sd[:])
-            nc.vector.reciprocal(out=sd[:], in_=sd[:])
-            nc.vector.tensor_mul(out=inv[:], in0=gam[:], in1=sd[:])
-            mi = small.tile([P, T], F32)
+            nc.vector.tensor_scalar_add(out=ve[:], in0=mv[:, :, 1], scalar1=EPS)
+            nc.gpsimd.tensor_tensor(out=rsd[:], in0=ve[:], in1=mhalf[:], op=ALU.pow)
+            nc.vector.tensor_mul(out=inv[:], in0=gam[:], in1=rsd[:])
             nc.vector.tensor_mul(out=mi[:], in0=mv[:, :, 0], in1=inv[:])
             nc.vector.tensor_sub(out=shift[:], in0=bet[:], in1=mi[:])
 
-        with ExitStack() as pb:
-            rpool = pb.enter_context(tc.tile_pool(name="rpool", bufs=4))
-            opool = pb.enter_context(tc.tile_pool(name="opool", bufs=3))
-            ps_c = pb.enter_context(tc.psum_pool(name="ps_c", bufs=4))
-            ps_s = pb.enter_context(tc.psum_pool(name="ps_s", bufs=4))
-            for q in range(PAIRS):
-                cols = slice(q * 2 * N, (q + 1) * 2 * N)
-                o_sb = opool.tile([P, 2, T, N], F32)
-                for a in range(T):
-                    y2 = ps_c.tile([P, 2 * N], F32)
-                    nc.tensor.matmul_mx(
-                        out=y2[:],
-                        lhsT=wq[:, a * P:(a + 1) * P].bitcast(FP8X4),
-                        lhsT_scale=ws[:, a * P:(a + 1) * P],
-                        rhs=xq[:, cols].bitcast(FP8X4),
-                        rhs_scale=xs[:, cols],
-                        start=True,
-                        stop=True,
-                    )
-                    sp = ps_s.tile([P, 2, N], F32)
-                    for j in range(2):
-                        b = 2 * q + j
-                        nc.tensor.matmul_mx(
-                            out=sp[:, j, :],
-                            lhsT=aq[:, b * C + a * P:b * C + (a + 1) * P].bitcast(FP8X4),
-                            lhsT_scale=asc[:, b * C + a * P:b * C + (a + 1) * P],
-                            rhs=xq[:, b * N:(b + 1) * N].bitcast(FP8X4),
-                            rhs_scale=xs[:, b * N:(b + 1) * N],
-                            start=True,
-                            stop=True,
-                        )
-                    r = rpool.tile([P, 2, N], F32)
-                    nc.scalar.activation(
-                        out=r[:].rearrange("p j n -> p (j n)"),
-                        in_=y2[:],
-                        func=ACT.Relu,
-                        bias=shift[:, a:a + 1],
-                        scale=inv[:, a:a + 1],
-                    )
-                    nc.vector.tensor_tensor(out=o_sb[:, :, a, :], in0=sp[:], in1=r[:], op=ALU.add)
+        load_group(0, [(0, 1), (1, 2)])
+        nc.sync.dma_start(out=w_sb[:].rearrange("m a c -> m (a c)"), in_=w_v)
+        flat0 = xgrp[0][:].rearrange("p b t n -> p b (t n)")
+        nc.sync.dma_start(out=flat0[:, 2:4, :], in_=x_v[:, 2:4, :])
+        for k in range(1, 5):
+            load_group(k, [(0, GROUP)])
+        nc.scalar.dma_start(out=gam_b[:], in_=gamma.rearrange("(m a) -> m a", a=T))
+        nc.scalar.dma_start(out=bet_b[:], in_=beta.rearrange("(m a) -> m a", a=T))
+        make_identity(nc, ident[:])
+        make_identity(nc, ident32[:])
+        nc.gpsimd.memset(mhalf[:], -0.5)
+
+        for i in range(-2, B + 2):
+            exq(i, 0)
+            gm(i + 1, 0)
+            xr(i + 2)
+            bs(2 * i - 2)
+            cv(2 * i - 1)
+            exq(i, 1)
+            gm(i + 1, 1)
+            nrm(i - 1, 2)
+            nrm(i - 1, 3)
+            mx(i + 1, 0)
+            mx(i + 1, 1)
+            ae(i - 2, 1)
+            tx(i + 2)
+            if i == 0:
+                w_transposes()
+            if i == 2:
+                load_group(5, [(0, GROUP)])
+            if i == 6:
+                load_group(6, [(0, GROUP)])
+            ta(i - 1, 0)
+            exq(i, 2)
+            gm(i + 1, 2)
+            qa(i - 2)
+            if i == 0:
+                w_quantise()
+            bs(2 * i - 1)
+            cv(2 * i)
+            exq(i, 3)
+            gm(i + 1, 3)
+            mx(i + 1, 2)
+            rc(i)
+            nrm(i, 0)
+            nrm(i, 1)
+            if i % 2 != 0:
+                qx((i + 1) // 2)
+            mx(i + 1, 3)
+            if i == 1:
+                nc.vector.tensor_copy(out=gam[:], in_=gam_b[:])
+                nc.vector.tensor_copy(out=bet[:], in_=bet_b[:])
+            if 2 * i == UNITS:
+                bn_constants()
+            ae(i - 1, 0)
+            xe(i + 2)
+            ta(i - 1, 1)
+
+        y_tags = [(ps_x, "x"), (ps_y, "y"), (ps_t, "pt"), (ps_t, "pt")]
+        o_sb = None
+        for u in range(UNITS):
+            q = u // T
+            a = u % T
+            if a == 0:
+                o_sb = big.tile([P, 2, T, N], F32, name="o_sb", tag="big")
+            ypool, ytag = y_tags[u % 4]
+            y2 = ypool.tile([P, 2 * N], F32, name="y2", tag=ytag)
+            conv(y2[:], q, a)
+            sp = ps_g.tile([P, 2, N], F32, name="sp", tag="g")
+            for j in range(2):
+                b = 2 * q + j
+                nc.tensor.matmul_mx(
+                    out=sp[:, j, :],
+                    lhsT=aq[:, b * C + a * P:b * C + (a + 1) * P].bitcast(FP8X4),
+                    lhsT_scale=asc[:, b * C + a * P:b * C + (a + 1) * P],
+                    rhs=xq[:, b * N:(b + 1) * N].bitcast(FP8X4),
+                    rhs_scale=xs[:, b * N:(b + 1) * N],
+                    start=True,
+                    stop=True,
+                )
+            r = epool.tile([P, 2, N], F32, name="r", tag="e")
+            nc.scalar.activation(
+                out=r[:].rearrange("p j n -> p (j n)"),
+                in_=y2[:],
+                func=ACT.Relu,
+                bias=shift[:, a:a + 1],
+                scale=inv[:, a:a + 1],
+            )
+            nc.vector.tensor_tensor(out=o_sb[:, :, a, :], in0=sp[:], in1=r[:], op=ALU.add)
+            if a == T - 1:
                 nc.sync.dma_start(
                     out=out_v[:, 2 * q:2 * q + 2, :], in_=o_sb[:].rearrange("p j a n -> p j (a n)")
                 )

@@ -238,20 +238,25 @@ def tile_informationinteraction_t_kernel(tc, x, conv_w, gamma, beta, out):
                 return
             nc.vector.bn_stats(out=st[:, u % T, u // T, :], in_=y_ps[u][:])
 
+        wt_ps = {}
+
         def w_transposes():
             w32 = w_sb[:].bitcast(F32).rearrange("m a (p u) -> m a u p", u=2)
+            for k in range(2):
+                wt_ps[k] = ps_t.tile([P, 2, 2, P], F32, name="wt", tag="pt")
+                for a2 in range(2):
+                    for u in range(2):
+                        nc.tensor.transpose(
+                            out=wt_ps[k][:, a2, u, :], in_=w32[:, 2 * k + a2, u, :], identity=ident32[:]
+                        )
+
+        def w_copies():
             g32 = w_grp[:].rearrange("p a m t -> p a (m t)").bitcast(F32).rearrange(
                 "p a (m u) -> p a m u", u=2
             )
             for k in range(2):
-                wt = ps_t.tile([P, 2, 2, P], F32, name="wt", tag="pt")
-                for a2 in range(2):
-                    for u in range(2):
-                        nc.tensor.transpose(
-                            out=wt[:, a2, u, :], in_=w32[:, 2 * k + a2, u, :], identity=ident32[:]
-                        )
                 nc.vector.tensor_copy(
-                    out=g32[:, 2 * k:2 * k + 2], in_=wt[:].rearrange("p a u m -> p a m u")
+                    out=g32[:, 2 * k:2 * k + 2], in_=wt_ps[k][:].rearrange("p a u m -> p a m u")
                 )
 
         def w_quantise():
@@ -282,51 +287,53 @@ def tile_informationinteraction_t_kernel(tc, x, conv_w, gamma, beta, out):
         make_identity(nc, ident32[:])
         nc.gpsimd.memset(mhalf[:], -0.5)
 
-        for i in range(-2, B + 2):
+        for i in range(-4, B + 3):
             exq(i, 0)
-            gm(i + 1, 0)
-            xr(i + 2)
-            bs(2 * i - 2)
-            cv(2 * i - 1)
-            exq(i, 1)
-            gm(i + 1, 1)
             nrm(i - 1, 2)
-            nrm(i - 1, 3)
-            mx(i + 1, 0)
-            mx(i + 1, 1)
-            ae(i - 2, 1)
-            tx(i + 2)
-            if i == 0:
-                w_transposes()
-            if i == 2:
-                load_group(5, [(0, GROUP)])
-            if i == 6:
-                load_group(6, [(0, GROUP)])
-            ta(i - 1, 0)
-            exq(i, 2)
-            gm(i + 1, 2)
-            qa(i - 2)
-            if i == 0:
-                w_quantise()
-            bs(2 * i - 1)
-            cv(2 * i)
-            exq(i, 3)
-            gm(i + 1, 3)
-            mx(i + 1, 2)
-            rc(i)
-            nrm(i, 0)
-            nrm(i, 1)
+            bs(2 * i)
+            exq(i, 1)
+            gm(i + 1, 0)
+            qa(i - 3)
             if i % 2 != 0:
                 qx((i + 1) // 2)
+            exq(i, 2)
+            tx(i + 2)
+            if i == -1:
+                w_transposes()
+            xr(i + 4)
+            exq(i, 3)
+            ta(i - 1, 0)
+            ae(i - 2, 1)
+            cv(2 * i + 1)
+            rc(i)
+            mx(i + 1, 0)
+            if i == -1:
+                w_copies()
+            gm(i + 1, 1)
+            nrm(i, 0)
+            bs(2 * i + 1)
+            gm(i + 1, 2)
+            xe(i + 2)
+            nrm(i, 1)
+            mx(i + 1, 1)
+            if i == -1:
+                w_quantise()
+            gm(i + 1, 3)
+            ae(i - 1, 0)
+            mx(i + 1, 2)
+            cv(2 * i + 2)
+            nrm(i, 3)
+            ta(i - 1, 1)
             mx(i + 1, 3)
             if i == 1:
                 nc.vector.tensor_copy(out=gam[:], in_=gam_b[:])
                 nc.vector.tensor_copy(out=bet[:], in_=bet_b[:])
-            if 2 * i == UNITS:
+            if i == 2:
+                load_group(5, [(0, GROUP)])
+            if i == 6:
+                load_group(6, [(0, GROUP)])
+            if i == B - 1:
                 bn_constants()
-            ae(i - 1, 0)
-            xe(i + 2)
-            ta(i - 1, 1)
 
         y_tags = [(ps_x, "x"), (ps_y, "y"), (ps_t, "pt"), (ps_t, "pt")]
         o_sb = None

@@ -21,6 +21,8 @@ EPS = 1e-5
 PAIRS = B // 2
 UNITS = PAIRS * T
 GROUP = 4
+XE_PERIOD = 4
+XE_PHASE = 2
 FLOPS = 3 * 2 * B * C * C * N
 
 
@@ -102,11 +104,14 @@ def tile_informationinteraction_t_kernel(tc, x, conv_w, gamma, beta, out):
                         identity=ident[:],
                     )
 
-        def xe(b):
-            if not 0 <= b < B:
+        def xe(b, on_vector):
+            if not 0 <= b < B or on_vector != (b % XE_PERIOD == XE_PHASE):
                 return
             xT[b] = work.tile([P, 2, C], BF16, name="xT", tag="xT")
-            nc.scalar.copy(out=xT[b][:], in_=xt_ps[b][:])
+            if on_vector:
+                nc.vector.tensor_copy(out=xT[b][:], in_=xt_ps[b][:])
+            else:
+                nc.scalar.copy(out=xT[b][:], in_=xt_ps[b][:])
 
         def gm(b, a):
             if not 0 <= b < B:
@@ -255,7 +260,7 @@ def tile_informationinteraction_t_kernel(tc, x, conv_w, gamma, beta, out):
                 "p a (m u) -> p a m u", u=2
             )
             for k in range(2):
-                nc.vector.tensor_copy(
+                nc.scalar.copy(
                     out=g32[:, 2 * k:2 * k + 2], in_=wt_ps[k][:].rearrange("p a u m -> p a m u")
                 )
 
@@ -275,9 +280,10 @@ def tile_informationinteraction_t_kernel(tc, x, conv_w, gamma, beta, out):
             nc.vector.tensor_mul(out=mi[:], in0=mv[:, :, 0], in1=inv[:])
             nc.vector.tensor_sub(out=shift[:], in0=bet[:], in1=mi[:])
 
-        load_group(0, [(0, 1), (1, 2)])
+        load_group(0, [(0, 1)])
         nc.sync.dma_start(out=w_sb[:].rearrange("m a c -> m (a c)"), in_=w_v)
         flat0 = xgrp[0][:].rearrange("p b t n -> p b (t n)")
+        nc.sync.dma_start(out=flat0[:, 1:2, :], in_=x_v[:, 1:2, :])
         nc.sync.dma_start(out=flat0[:, 2:4, :], in_=x_v[:, 2:4, :])
         for k in range(1, 5):
             load_group(k, [(0, GROUP)])
@@ -298,7 +304,7 @@ def tile_informationinteraction_t_kernel(tc, x, conv_w, gamma, beta, out):
                 qx((i + 1) // 2)
             exq(i, 2)
             tx(i + 2)
-            if i == -1:
+            if i == -2:
                 w_transposes()
             xr(i + 4)
             exq(i, 3)
@@ -306,18 +312,19 @@ def tile_informationinteraction_t_kernel(tc, x, conv_w, gamma, beta, out):
             ae(i - 2, 1)
             cv(2 * i + 1)
             rc(i)
+            xe(i + 2, True)
             mx(i + 1, 0)
             if i == -1:
-                w_copies()
+                w_quantise()
             gm(i + 1, 1)
             nrm(i, 0)
             bs(2 * i + 1)
             gm(i + 1, 2)
-            xe(i + 2)
+            xe(i + 2, False)
+            if i == -2:
+                w_copies()
             nrm(i, 1)
             mx(i + 1, 1)
-            if i == -1:
-                w_quantise()
             gm(i + 1, 3)
             ae(i - 1, 0)
             mx(i + 1, 2)
@@ -366,7 +373,8 @@ def tile_informationinteraction_t_kernel(tc, x, conv_w, gamma, beta, out):
                 scale=inv[:, a:a + 1],
             )
             nc.vector.tensor_tensor(out=o_sb[:, :, a, :], in0=sp[:], in1=r[:], op=ALU.add)
-            if a == T - 1:
+            if a % 2 == 1:
                 nc.sync.dma_start(
-                    out=out_v[:, 2 * q:2 * q + 2, :], in_=o_sb[:].rearrange("p j a n -> p j (a n)")
+                    out=out_v[:, 2 * q:2 * q + 2, (a - 1) * N:(a + 1) * N],
+                    in_=o_sb[:, :, a - 1:a + 1, :].rearrange("p j a n -> p j (a n)"),
                 )

@@ -21,8 +21,6 @@ EPS = 1e-5
 PAIRS = B // 2
 UNITS = PAIRS * T
 GROUP = 4
-XE_PERIOD = 4
-XE_PHASE = 2
 FLOPS = 3 * 2 * B * C * C * N
 
 
@@ -104,14 +102,11 @@ def tile_informationinteraction_t_kernel(tc, x, conv_w, gamma, beta, out):
                         identity=ident[:],
                     )
 
-        def xe(b, on_vector):
-            if not 0 <= b < B or on_vector != (b % XE_PERIOD == XE_PHASE):
+        def xe(b):
+            if not 0 <= b < B:
                 return
             xT[b] = work.tile([P, 2, C], BF16, name="xT", tag="xT")
-            if on_vector:
-                nc.vector.tensor_copy(out=xT[b][:], in_=xt_ps[b][:])
-            else:
-                nc.scalar.copy(out=xT[b][:], in_=xt_ps[b][:])
+            nc.scalar.copy(out=xT[b][:].bitcast(F32), in_=xt_ps[b][:].bitcast(F32))
 
         def gm(b, a):
             if not 0 <= b < B:
@@ -142,8 +137,8 @@ def tile_informationinteraction_t_kernel(tc, x, conv_w, gamma, beta, out):
                 ssum[b] = small.tile([P, T], F32, name="ssum", tag="ssum")
             ex[b, a] = epool.tile([P, C], F32, name="ex", tag="e")
             nc.scalar.activation(
-                out=ex[b, a][:],
-                in_=g_ps[b, a][:],
+                out=ex[b, a][:].rearrange("p (u q e) -> p u q e", u=2, e=2),
+                in_=g_ps[b, a][:].rearrange("p (u e q) -> p u q e", u=2, e=2),
                 func=ACT.Exp,
                 bias=nm[b][:, a:a + 1],
                 scale=1.0,
@@ -172,13 +167,14 @@ def tile_informationinteraction_t_kernel(tc, x, conv_w, gamma, beta, out):
         def ta(b, k):
             if not 0 <= b < B:
                 return
-            pt[b, k] = ps_t.tile([P, 2, T, P], BF16, name="pt", tag="pt")
+            pt[b, k] = ps_t.tile([P, 2, 2, P], F32, name="pt", tag="pt")
             for a2 in range(2):
-                for t in range(T):
+                words = att[b, 2 * k + a2][:].bitcast(F32)
+                for u in range(2):
                     nc.tensor.transpose(
-                        out=pt[b, k][:, a2, t, :],
-                        in_=att[b, 2 * k + a2][:, t * P:(t + 1) * P],
-                        identity=ident[:],
+                        out=pt[b, k][:, a2, u, :],
+                        in_=words[:, u * P:(u + 1) * P],
+                        identity=ident32[:],
                     )
 
         def ae(b, k):
@@ -186,9 +182,12 @@ def tile_informationinteraction_t_kernel(tc, x, conv_w, gamma, beta, out):
                 return
             if k == 0:
                 ag[b] = work.tile([P, T, P, T], BF16, name="ag", tag="ag", align_bytes=64)
+            words = ag[b][:].rearrange("p a m t -> p a (m t)").bitcast(F32).rearrange(
+                "p a (m u) -> p a m u", u=2
+            )
             nc.scalar.copy(
-                out=ag[b][:, 2 * k:2 * k + 2, :, :],
-                in_=pt[b, k][:].rearrange("p a t m -> p a m t"),
+                out=words[:, 2 * k:2 * k + 2],
+                in_=pt[b, k][:].rearrange("p a u m -> p a m u"),
             )
 
         def qa(b):
@@ -312,7 +311,6 @@ def tile_informationinteraction_t_kernel(tc, x, conv_w, gamma, beta, out):
             ae(i - 2, 1)
             cv(2 * i + 1)
             rc(i)
-            xe(i + 2, True)
             mx(i + 1, 0)
             if i == -1:
                 w_quantise()
@@ -320,7 +318,7 @@ def tile_informationinteraction_t_kernel(tc, x, conv_w, gamma, beta, out):
             nrm(i, 0)
             bs(2 * i + 1)
             gm(i + 1, 2)
-            xe(i + 2, False)
+            xe(i + 2)
             if i == -2:
                 w_copies()
             nrm(i, 1)

@@ -20,26 +20,35 @@ T = 4
 EPS = 1e-5
 PAIRS = B // 2
 UNITS = PAIRS * T
-GROUP = 4
+XIN = 8
 FLOPS = 3 * 2 * B * C * C * N
+
+PREP = -2
+OUT_FIRST = 64
+OUT_SKIP = 6
+FIRST = -2
+LAST = 4 * B + 24
 
 
 def tile_informationinteraction_t_kernel(tc, x, conv_w, gamma, beta, out):
     nc = tc.nc
-    x_v = x.rearrange("b (p t) h w -> p b (t h w)", t=T)
-    out_v = out.rearrange("b (m a) h w -> m b (a h w)", a=T)
-    w_v = conv_w.rearrange("(m a) c -> m (a c)", a=T)
+    x_v = x.rearrange("b (s q) h w -> b q s (h w)", q=P)
+    out_v = out.rearrange("b (a m) h w -> a m b (h w)", a=T)
+    w_v = conv_w.rearrange("(a m) c -> m a c", a=T)
 
     with ExitStack() as ctx:
         keep = ctx.enter_context(tc.tile_pool(name="keep", bufs=1))
-        big = ctx.enter_context(tc.tile_pool(name="big", bufs=5))
+        xin = ctx.enter_context(tc.tile_pool(name="xin", bufs=XIN))
+        xtp = ctx.enter_context(tc.tile_pool(name="xtp", bufs=16))
         work = ctx.enter_context(tc.tile_pool(name="work", bufs=2))
-        epool = ctx.enter_context(tc.tile_pool(name="epool", bufs=8))
+        epool = ctx.enter_context(tc.tile_pool(name="epool", bufs=10))
+        apool = ctx.enter_context(tc.tile_pool(name="apool", bufs=8))
+        opool = ctx.enter_context(tc.tile_pool(name="opool", bufs=4))
         small = ctx.enter_context(tc.tile_pool(name="small", bufs=4))
-        ps_g = ctx.enter_context(tc.psum_pool(name="ps_g", bufs=4))
-        ps_t = ctx.enter_context(tc.psum_pool(name="ps_t", bufs=2))
-        ps_x = ctx.enter_context(tc.psum_pool(name="ps_x", bufs=1))
-        ps_y = ctx.enter_context(tc.psum_pool(name="ps_y", bufs=1))
+        ps_g = ctx.enter_context(tc.psum_pool(name="ps_g", bufs=3))
+        ps_x = ctx.enter_context(tc.psum_pool(name="ps_x", bufs=2))
+        ps_y = ctx.enter_context(tc.psum_pool(name="ps_y", bufs=2))
+        ps_t = ctx.enter_context(tc.psum_pool(name="ps_t", bufs=1))
         ctx.enter_context(tc.manual_schedule())
 
         ident = keep.tile([P, P], BF16, name="ident")
@@ -55,19 +64,20 @@ def tile_informationinteraction_t_kernel(tc, x, conv_w, gamma, beta, out):
         mv = keep.tile([P, T, 2], F32, name="mv")
         inv = keep.tile([P, T], F32, name="inv")
         shift = keep.tile([P, T], F32, name="shift")
-        gam_b = keep.tile([P, T], BF16, name="gam_b")
-        bet_b = keep.tile([P, T], BF16, name="bet_b")
-        gam = keep.tile([P, T], F32, name="gam")
-        bet = keep.tile([P, T], F32, name="bet")
+        gb = keep.tile([P, P], BF16, name="gb")
+        gbt = keep.tile([P, 2 * T], F32, name="gbt")
         ve = keep.tile([P, T], F32, name="ve")
         rsd = keep.tile([P, T], F32, name="rsd")
         mi = keep.tile([P, T], F32, name="mi")
         w_sb = keep.tile([P, T, C], BF16, name="w_sb")
         w_grp = keep.tile([P, T, P, T], BF16, name="w_grp", align_bytes=64)
 
-        xgrp = {}
+        xn = {}
         xt_ps = {}
         xT = {}
+        xg_ps = {}
+        xg = {}
+        y_ps = {}
         g_ps = {}
         nm = {}
         ssum = {}
@@ -76,142 +86,49 @@ def tile_informationinteraction_t_kernel(tc, x, conv_w, gamma, beta, out):
         att = {}
         pt = {}
         ag = {}
-        xg = {}
-        y_ps = {}
 
-        def load_group(k, cuts):
-            xgrp[k] = big.tile([P, GROUP, T, N], BF16, name="xgrp", tag="big")
-            flat = xgrp[k][:].rearrange("p b t n -> p b (t n)")
-            for lo, hi in cuts:
-                nc.sync.dma_start(
-                    out=flat[:, lo:hi, :], in_=x_v[:, k * GROUP + lo:k * GROUP + hi, :]
-                )
-
-        def x_of(b):
-            return xgrp[b // GROUP][:, b % GROUP]
+        def load_x(b):
+            if b >= B:
+                return
+            xn[b] = xin.tile([P, T, N], BF16, name="xn", tag="xn")
+            nc.sync.dma_start(out=xn[b][:], in_=x_v[b])
 
         def tx(b):
-            if not 0 <= b < B:
-                return
             xt_ps[b] = ps_x.tile([P, 2, C], BF16, name="xt_ps", tag="x")
             for h in range(2):
-                for t in range(T):
+                for s in range(T):
                     nc.tensor.transpose(
-                        out=xt_ps[b][:, h, t * P:(t + 1) * P],
-                        in_=x_of(b)[:, t, h * P:(h + 1) * P],
+                        out=xt_ps[b][:, h, s * P:(s + 1) * P],
+                        in_=xn[b][:, s, h * P:(h + 1) * P],
                         identity=ident[:],
                     )
+            load_x(b + XIN)
 
         def xe(b):
-            if not 0 <= b < B:
-                return
-            xT[b] = work.tile([P, 2, C], BF16, name="xT", tag="xT")
+            xT[b] = xtp.tile([P, 2, C], BF16, name="xT", tag="xT")
             nc.scalar.copy(out=xT[b][:].bitcast(F32), in_=xt_ps[b][:].bitcast(F32))
 
-        def gm(b, a):
-            if not 0 <= b < B:
-                return
-            g_ps[b, a] = ps_g.tile([P, C], F32, name="g_ps", tag="g")
+        def tg(b):
+            xg_ps[b] = ps_x.tile([P, 2, 2, P], F32, name="xg_ps", tag="x")
+            words = xT[b][:].bitcast(F32)
             for h in range(2):
-                nc.tensor.matmul(
-                    out=g_ps[b, a][:],
-                    lhsT=xT[b][:, h, a * P:(a + 1) * P],
-                    rhs=xT[b][:, h, :],
-                    start=(h == 0),
-                    stop=(h == 1),
-                )
-
-        def mx(b, a):
-            if not 0 <= b < B:
-                return
-            if a == 0:
-                nm[b] = small.tile([P, T], F32, name="nm", tag="nm")
-            nc.vector.tensor_reduce(
-                out=nm[b][:, a:a + 1], in_=g_ps[b, a][:], axis=AX.X, op=ALU.max, negate=True
-            )
-
-        def exq(b, a):
-            if not 0 <= b < B:
-                return
-            if a == 0:
-                ssum[b] = small.tile([P, T], F32, name="ssum", tag="ssum")
-            ex[b, a] = epool.tile([P, C], F32, name="ex", tag="e")
-            nc.scalar.activation(
-                out=ex[b, a][:].rearrange("p (u q e) -> p u q e", u=2, e=2),
-                in_=g_ps[b, a][:].rearrange("p (u e q) -> p u q e", u=2, e=2),
-                func=ACT.Exp,
-                bias=nm[b][:, a:a + 1],
-                scale=1.0,
-                accum_out=ssum[b][:, a:a + 1],
-            )
-
-        def rc(b):
-            if not 0 <= b < B:
-                return
-            rs[b] = small.tile([P, T], F32, name="rs", tag="rs")
-            nc.vector.reciprocal(out=rs[b][:], in_=ssum[b][:])
-
-        def nrm(b, a):
-            if not 0 <= b < B:
-                return
-            att[b, a] = epool.tile([P, C], BF16, name="att", tag="att")
-            nc.gpsimd.tensor_scalar(
-                out=att[b, a][:],
-                in0=ex[b, a][:],
-                scalar1=rs[b][:, a:a + 1],
-                scalar2=0.0,
-                op0=ALU.mult,
-                op1=ALU.add,
-            )
-
-        def ta(b, k):
-            if not 0 <= b < B:
-                return
-            pt[b, k] = ps_t.tile([P, 2, 2, P], F32, name="pt", tag="pt")
-            for a2 in range(2):
-                words = att[b, 2 * k + a2][:].bitcast(F32)
                 for u in range(2):
                     nc.tensor.transpose(
-                        out=pt[b, k][:, a2, u, :],
-                        in_=words[:, u * P:(u + 1) * P],
+                        out=xg_ps[b][:, h, u, :],
+                        in_=words[:, h, u * P:(u + 1) * P],
                         identity=ident32[:],
                     )
 
-        def ae(b, k):
-            if not 0 <= b < B:
-                return
-            if k == 0:
-                ag[b] = work.tile([P, T, P, T], BF16, name="ag", tag="ag", align_bytes=64)
-            words = ag[b][:].rearrange("p a m t -> p a (m t)").bitcast(F32).rearrange(
-                "p a (m u) -> p a m u", u=2
-            )
-            nc.scalar.copy(
-                out=words[:, 2 * k:2 * k + 2],
-                in_=pt[b, k][:].rearrange("p a u m -> p a m u"),
-            )
-
-        def qa(b):
-            if not 0 <= b < B:
-                return
-            nc.vector.quantize_mx(
-                out=aq[:, b * C:(b + 1) * C].bitcast(FP8X4),
-                scales=asc[:, b * C:(b + 1) * C],
-                in_=ag[b][:].rearrange("p a m t -> p (a m t)"),
-            )
-
-        def xr(b):
-            if not 0 <= b < B:
-                return
+        def xge(b):
             if b % 2 == 0:
                 xg[b // 2] = work.tile([P, 2, N, T], BF16, name="xg", tag="xg", align_bytes=64)
-            nc.vector.tensor_copy(
-                out=xg[b // 2][:, b % 2].rearrange("p (c i) t -> p c t i", i=4),
-                in_=x_of(b).rearrange("p t (c i) -> p c t i", i=4),
+            words = xg[b // 2][:, b % 2].rearrange("p n t -> p (n t)").bitcast(F32)
+            nc.scalar.copy(
+                out=words.rearrange("p (h n u) -> p h n u", h=2, u=2),
+                in_=xg_ps[b][:].rearrange("p h u n -> p h n u"),
             )
 
         def qx(q):
-            if not 0 <= q < PAIRS:
-                return
             cols = slice(q * 2 * N, (q + 1) * 2 * N)
             nc.vector.quantize_mx(
                 out=xq[:, cols].bitcast(FP8X4),
@@ -232,125 +149,139 @@ def tile_informationinteraction_t_kernel(tc, x, conv_w, gamma, beta, out):
             )
 
         def cv(u):
-            if not 0 <= u < UNITS:
-                return
             y_ps[u] = ps_y.tile([P, 2 * N], F32, name="y_ps", tag="y")
             conv(y_ps[u][:], u // T, u % T)
 
         def bs(u):
-            if not 0 <= u < UNITS:
-                return
             nc.vector.bn_stats(out=st[:, u % T, u // T, :], in_=y_ps[u][:])
 
-        wt_ps = {}
+        def gm(k):
+            b, a = divmod(k, T)
+            g_ps[k] = ps_g.tile([P, C], F32, name="g_ps", tag="g")
+            for h in range(2):
+                nc.tensor.matmul(
+                    out=g_ps[k][:],
+                    lhsT=xT[b][:, h, a * P:(a + 1) * P],
+                    rhs=xT[b][:, h, :],
+                    start=(h == 0),
+                    stop=(h == 1),
+                )
 
-        def w_transposes():
-            w32 = w_sb[:].bitcast(F32).rearrange("m a (p u) -> m a u p", u=2)
-            for k in range(2):
-                wt_ps[k] = ps_t.tile([P, 2, 2, P], F32, name="wt", tag="pt")
-                for a2 in range(2):
-                    for u in range(2):
-                        nc.tensor.transpose(
-                            out=wt_ps[k][:, a2, u, :], in_=w32[:, 2 * k + a2, u, :], identity=ident32[:]
-                        )
+        def mx(k):
+            b, a = divmod(k, T)
+            if a == 0:
+                nm[b] = small.tile([P, T], F32, name="nm", tag="nm")
+            nc.vector.tensor_reduce(
+                out=nm[b][:, a:a + 1], in_=g_ps[k][:], axis=AX.X, op=ALU.max, negate=True
+            )
 
-        def w_copies():
+        def exq(k):
+            b, a = divmod(k, T)
+            if a == 0:
+                ssum[b] = small.tile([P, T], F32, name="ssum", tag="ssum")
+            ex[k] = epool.tile([P, C], F32, name="ex", tag="e")
+            nc.scalar.activation(
+                out=ex[k][:],
+                in_=g_ps[k][:],
+                func=ACT.Exp,
+                bias=nm[b][:, a:a + 1],
+                scale=1.0,
+                accum_out=ssum[b][:, a:a + 1],
+            )
+
+        def rc(b):
+            rs[b] = small.tile([P, T], F32, name="rs", tag="rs")
+            nc.vector.reciprocal(out=rs[b][:], in_=ssum[b][:])
+
+        def nrm(b):
+            for a in range(T):
+                att[b, a] = apool.tile([P, C], BF16, name="att", tag="att")
+                nc.gpsimd.tensor_scalar(
+                    out=att[b, a][:],
+                    in0=ex[b * T + a][:],
+                    scalar1=rs[b][:, a:a + 1],
+                    scalar2=0.0,
+                    op0=ALU.mult,
+                    op1=ALU.add,
+                )
+
+        def ta(k):
+            b, half = divmod(k, 2)
+            pt[k] = ps_t.tile([P, 2, 2, P], F32, name="pt", tag="pt")
+            for a2 in range(2):
+                words = att[b, 2 * half + a2][:].bitcast(F32)
+                for u in range(2):
+                    nc.tensor.transpose(
+                        out=pt[k][:, a2, u, :],
+                        in_=words[:, u * P:(u + 1) * P],
+                        identity=ident32[:],
+                    )
+
+        def ae(k):
+            b, half = divmod(k, 2)
+            if half == 0:
+                ag[b] = work.tile([P, T, P, T], BF16, name="ag", tag="ag", align_bytes=64)
+            words = ag[b][:].rearrange("p a m t -> p a (m t)").bitcast(F32).rearrange(
+                "p a (m u) -> p a m u", u=2
+            )
+            nc.scalar.copy(
+                out=words[:, 2 * half:2 * half + 2],
+                in_=pt[k][:].rearrange("p a u m -> p a m u"),
+            )
+
+        def qa(b):
+            nc.vector.quantize_mx(
+                out=aq[:, b * C:(b + 1) * C].bitcast(FP8X4),
+                scales=asc[:, b * C:(b + 1) * C],
+                in_=ag[b][:].rearrange("p a m t -> p (a m t)"),
+            )
+
+        def prepare_w():
+            w32 = w_sb[:].bitcast(F32)
             g32 = w_grp[:].rearrange("p a m t -> p a (m t)").bitcast(F32).rearrange(
                 "p a (m u) -> p a m u", u=2
             )
             for k in range(2):
+                wt = ps_y.tile([P, 2, 2, P], F32, name="wt", tag="y")
+                for a2 in range(2):
+                    for u in range(2):
+                        nc.tensor.transpose(
+                            out=wt[:, a2, u, :],
+                            in_=w32[:, 2 * k + a2, u * P:(u + 1) * P],
+                            identity=ident32[:],
+                        )
                 nc.scalar.copy(
-                    out=g32[:, 2 * k:2 * k + 2], in_=wt_ps[k][:].rearrange("p a u m -> p a m u")
+                    out=g32[:, 2 * k:2 * k + 2], in_=wt[:].rearrange("p a u m -> p a m u")
                 )
 
-        def w_quantise():
+        def quantise_w():
             nc.vector.quantize_mx(
                 out=wq[:].bitcast(FP8X4),
                 scales=ws[:],
                 in_=w_grp[:].rearrange("p a m t -> p (a m t)"),
             )
 
-        def bn_constants():
+        def spread_gamma_beta():
+            gbp = ps_y.tile([P, P], BF16, name="gbp", tag="y")
+            nc.tensor.transpose(out=gbp[:], in_=gb[:], identity=ident[:])
+            nc.vector.tensor_copy(out=gbt[:], in_=gbp[:, 0:2 * T])
+
+        def bn_first():
             for a in range(T):
                 nc.vector.bn_aggr(out=mv[:, a, :], in_=st[:, a].rearrange("p q s -> p (q s)"))
             nc.vector.tensor_scalar_add(out=ve[:], in0=mv[:, :, 1], scalar1=EPS)
             nc.gpsimd.tensor_tensor(out=rsd[:], in0=ve[:], in1=mhalf[:], op=ALU.pow)
-            nc.vector.tensor_mul(out=inv[:], in0=gam[:], in1=rsd[:])
+
+        def bn_second():
+            nc.vector.tensor_mul(out=inv[:], in0=gbt[:, 0:T], in1=rsd[:])
             nc.vector.tensor_mul(out=mi[:], in0=mv[:, :, 0], in1=inv[:])
-            nc.vector.tensor_sub(out=shift[:], in0=bet[:], in1=mi[:])
+            nc.vector.tensor_sub(out=shift[:], in0=gbt[:, T:2 * T], in1=mi[:])
 
-        load_group(0, [(0, 1)])
-        nc.sync.dma_start(out=w_sb[:].rearrange("m a c -> m (a c)"), in_=w_v)
-        flat0 = xgrp[0][:].rearrange("p b t n -> p b (t n)")
-        nc.sync.dma_start(out=flat0[:, 1:2, :], in_=x_v[:, 1:2, :])
-        nc.sync.dma_start(out=flat0[:, 2:4, :], in_=x_v[:, 2:4, :])
-        for k in range(1, 5):
-            load_group(k, [(0, GROUP)])
-        nc.scalar.dma_start(out=gam_b[:], in_=gamma.rearrange("(m a) -> m a", a=T))
-        nc.scalar.dma_start(out=bet_b[:], in_=beta.rearrange("(m a) -> m a", a=T))
-        make_identity(nc, ident[:])
-        make_identity(nc, ident32[:])
-        nc.gpsimd.memset(mhalf[:], -0.5)
-
-        for i in range(-4, B + 3):
-            exq(i, 0)
-            nrm(i - 1, 2)
-            bs(2 * i)
-            exq(i, 1)
-            gm(i + 1, 0)
-            qa(i - 3)
-            if i % 2 != 0:
-                qx((i + 1) // 2)
-            exq(i, 2)
-            tx(i + 2)
-            if i == -2:
-                w_transposes()
-            xr(i + 4)
-            exq(i, 3)
-            ta(i - 1, 0)
-            ae(i - 2, 1)
-            cv(2 * i + 1)
-            rc(i)
-            mx(i + 1, 0)
-            if i == -1:
-                w_quantise()
-            gm(i + 1, 1)
-            nrm(i, 0)
-            bs(2 * i + 1)
-            gm(i + 1, 2)
-            xe(i + 2)
-            if i == -2:
-                w_copies()
-            nrm(i, 1)
-            mx(i + 1, 1)
-            gm(i + 1, 3)
-            ae(i - 1, 0)
-            mx(i + 1, 2)
-            cv(2 * i + 2)
-            nrm(i, 3)
-            ta(i - 1, 1)
-            mx(i + 1, 3)
-            if i == 1:
-                nc.vector.tensor_copy(out=gam[:], in_=gam_b[:])
-                nc.vector.tensor_copy(out=bet[:], in_=bet_b[:])
-            if i == 2:
-                load_group(5, [(0, GROUP)])
-            if i == 6:
-                load_group(6, [(0, GROUP)])
-            if i == B - 1:
-                bn_constants()
-
-        y_tags = [(ps_x, "x"), (ps_y, "y"), (ps_t, "pt"), (ps_t, "pt")]
-        o_sb = None
-        for u in range(UNITS):
-            q = u // T
-            a = u % T
-            if a == 0:
-                o_sb = big.tile([P, 2, T, N], F32, name="o_sb", tag="big")
-            ypool, ytag = y_tags[u % 4]
-            y2 = ypool.tile([P, 2 * N], F32, name="y2", tag=ytag)
+        def pb(u):
+            q, a = divmod(u, T)
+            y2 = ps_y.tile([P, 2 * N], F32, name="y2", tag="y")
             conv(y2[:], q, a)
-            sp = ps_g.tile([P, 2, N], F32, name="sp", tag="g")
+            sp = ps_x.tile([P, 2, N], F32, name="sp", tag="x")
             for j in range(2):
                 b = 2 * q + j
                 nc.tensor.matmul_mx(
@@ -362,7 +293,7 @@ def tile_informationinteraction_t_kernel(tc, x, conv_w, gamma, beta, out):
                     start=True,
                     stop=True,
                 )
-            r = epool.tile([P, 2, N], F32, name="r", tag="e")
+            r = opool.tile([P, 2, N], F32, name="r", tag="r")
             nc.scalar.activation(
                 out=r[:].rearrange("p j n -> p (j n)"),
                 in_=y2[:],
@@ -370,9 +301,57 @@ def tile_informationinteraction_t_kernel(tc, x, conv_w, gamma, beta, out):
                 bias=shift[:, a:a + 1],
                 scale=inv[:, a:a + 1],
             )
-            nc.vector.tensor_tensor(out=o_sb[:, :, a, :], in0=sp[:], in1=r[:], op=ALU.add)
-            if a % 2 == 1:
-                nc.sync.dma_start(
-                    out=out_v[:, 2 * q:2 * q + 2, (a - 1) * N:(a + 1) * N],
-                    in_=o_sb[:, :, a - 1:a + 1, :].rearrange("p j a n -> p j (a n)"),
-                )
+            o = opool.tile([P, 2, N], F32, name="o", tag="o")
+            nc.vector.tensor_tensor(out=o[:], in0=sp[:], in1=r[:], op=ALU.add)
+            nc.sync.dma_start(out=out_v[a, :, 2 * q:2 * q + 2, :], in_=o[:])
+
+        load_x(0)
+        load_x(1)
+        nc.sync.dma_start(out=w_sb[:], in_=w_v)
+        for b in range(2, XIN):
+            load_x(b)
+        make_identity(nc, ident[:])
+        make_identity(nc, ident32[:])
+        nc.gpsimd.memset(mhalf[:], -0.5)
+        nc.vector.memset(gb[:], 0.0)
+        nc.scalar.dma_start(out=gb[0:T, :], in_=gamma.rearrange("(a m) -> a m", a=T))
+        nc.scalar.dma_start(out=gb[T:2 * T, :], in_=beta.rearrange("(a m) -> a m", a=T))
+
+        def run(op, count, quarter, lag, period):
+            n, rest = divmod(quarter - lag, period)
+            if rest == 0 and 0 <= n < count:
+                op(n)
+
+        unit = 0
+        for Q in range(FIRST, LAST):
+            run(tx, B, Q, PREP, 2)
+            run(rc, B, Q, 5, 4)
+            run(qx, PAIRS, Q, PREP + 6, 4)
+            run(bs, UNITS, Q, PREP + 7, 1)
+            run(tg, B, Q, PREP + 2, 2)
+            run(ta, 2 * B, Q, 12, 2)
+            run(gm, 4 * B, Q, 0, 1)
+            run(nrm, B, Q, 6, 4)
+            run(xe, B, Q, PREP, 2)
+            run(mx, 4 * B, Q, 0, 1)
+            run(qa, B, Q, 16, 4)
+            run(ae, 2 * B, Q, 12, 2)
+            if Q == 0:
+                prepare_w()
+            if Q == 1:
+                quantise_w()
+                spread_gamma_beta()
+            if Q == OUT_FIRST - 3:
+                bn_first()
+            if Q == OUT_FIRST - 1:
+                bn_second()
+            while (
+                unit < UNITS
+                and Q >= OUT_FIRST + unit + unit // (OUT_SKIP - 1)
+                and Q > 4 * (2 * (unit // T) + 1) + 16
+            ):
+                pb(unit)
+                unit += 1
+            run(xge, B, Q, PREP + 3, 2)
+            run(cv, UNITS, Q, PREP + 6, 1)
+            run(exq, 4 * B, Q, 1, 1)

@@ -21,6 +21,7 @@ EPS = 1e-5
 PAIRS = B // 2
 UNITS = PAIRS * T
 XIN = 8
+XO_BUFS = 12
 FLOPS = 3 * 2 * B * C * C * N
 
 PREP = -2
@@ -38,7 +39,7 @@ def tile_informationinteraction_t_kernel(tc, x, conv_w, gamma, beta, out):
 
     with ExitStack() as ctx:
         keep = ctx.enter_context(tc.tile_pool(name="keep", bufs=1))
-        xin = ctx.enter_context(tc.tile_pool(name="xin", bufs=XIN))
+        xin = ctx.enter_context(tc.tile_pool(name="xin", bufs=XO_BUFS))
         xtp = ctx.enter_context(tc.tile_pool(name="xtp", bufs=16))
         work = ctx.enter_context(tc.tile_pool(name="work", bufs=2))
         epool = ctx.enter_context(tc.tile_pool(name="epool", bufs=10))
@@ -90,7 +91,7 @@ def tile_informationinteraction_t_kernel(tc, x, conv_w, gamma, beta, out):
         def load_x(b):
             if b >= B:
                 return
-            xn[b] = xin.tile([P, T, N], BF16, name="xn", tag="xn")
+            xn[b] = xin.tile([P, T, N], BF16, name="xn", tag="xo")
             nc.sync.dma_start(out=xn[b][:], in_=x_v[b])
 
         def tx(b):
@@ -301,7 +302,7 @@ def tile_informationinteraction_t_kernel(tc, x, conv_w, gamma, beta, out):
                 bias=shift[:, a:a + 1],
                 scale=inv[:, a:a + 1],
             )
-            o = opool.tile([P, 2, N], F32, name="o", tag="o")
+            o = xin.tile([P, 2, N], F32, name="o", tag="xo")
             nc.vector.tensor_tensor(out=o[:], in0=sp[:], in1=r[:], op=ALU.add)
             nc.sync.dma_start(out=out_v[a, :, 2 * q:2 * q + 2, :], in_=o[:])
 

@@ -24,11 +24,8 @@ XIN = 8
 XO_BUFS = 12
 FLOPS = 3 * 2 * B * C * C * N
 
-PREP = -2
-OUT_FIRST = 64
-OUT_SKIP = 6
-FIRST = -2
-LAST = 4 * B + 24
+PREP = -3
+LAST = 4 * B + 9
 
 
 def tile_informationinteraction_t_kernel(tc, x, conv_w, gamma, beta, out):
@@ -40,16 +37,16 @@ def tile_informationinteraction_t_kernel(tc, x, conv_w, gamma, beta, out):
     with ExitStack() as ctx:
         keep = ctx.enter_context(tc.tile_pool(name="keep", bufs=1))
         xin = ctx.enter_context(tc.tile_pool(name="xin", bufs=XO_BUFS))
-        xtp = ctx.enter_context(tc.tile_pool(name="xtp", bufs=16))
+        xtp = ctx.enter_context(tc.tile_pool(name="xtp", bufs=4))
         work = ctx.enter_context(tc.tile_pool(name="work", bufs=2))
-        epool = ctx.enter_context(tc.tile_pool(name="epool", bufs=10))
+        epool = ctx.enter_context(tc.tile_pool(name="epool", bufs=12))
         apool = ctx.enter_context(tc.tile_pool(name="apool", bufs=8))
         opool = ctx.enter_context(tc.tile_pool(name="opool", bufs=4))
         small = ctx.enter_context(tc.tile_pool(name="small", bufs=4))
-        ps_g = ctx.enter_context(tc.psum_pool(name="ps_g", bufs=3))
-        ps_x = ctx.enter_context(tc.psum_pool(name="ps_x", bufs=2))
-        ps_y = ctx.enter_context(tc.psum_pool(name="ps_y", bufs=2))
-        ps_t = ctx.enter_context(tc.psum_pool(name="ps_t", bufs=1))
+        ps_g = ctx.enter_context(tc.psum_pool(name="ps_g", bufs=4))
+        ps_x = ctx.enter_context(tc.psum_pool(name="ps_x", bufs=1))
+        ps_y = ctx.enter_context(tc.psum_pool(name="ps_y", bufs=1))
+        ps_t = ctx.enter_context(tc.psum_pool(name="ps_t", bufs=2))
         ctx.enter_context(tc.manual_schedule())
 
         ident = keep.tile([P, P], BF16, name="ident")
@@ -156,17 +153,22 @@ def tile_informationinteraction_t_kernel(tc, x, conv_w, gamma, beta, out):
         def bs(u):
             nc.vector.bn_stats(out=st[:, u % T, u // T, :], in_=y_ps[u][:])
 
-        def gm(k):
+        def gram_half(k, h):
             b, a = divmod(k, T)
+            nc.tensor.matmul(
+                out=g_ps[k][:],
+                lhsT=xT[b][:, h, a * P:(a + 1) * P],
+                rhs=xT[b][:, h, :],
+                start=(h == 0),
+                stop=(h == 1),
+            )
+
+        def gm1(k):
             g_ps[k] = ps_g.tile([P, C], F32, name="g_ps", tag="g")
-            for h in range(2):
-                nc.tensor.matmul(
-                    out=g_ps[k][:],
-                    lhsT=xT[b][:, h, a * P:(a + 1) * P],
-                    rhs=xT[b][:, h, :],
-                    start=(h == 0),
-                    stop=(h == 1),
-                )
+            gram_half(k, 0)
+
+        def gm2(k):
+            gram_half(k, 1)
 
         def mx(k):
             b, a = divmod(k, T)
@@ -243,7 +245,7 @@ def tile_informationinteraction_t_kernel(tc, x, conv_w, gamma, beta, out):
                 "p a (m u) -> p a m u", u=2
             )
             for k in range(2):
-                wt = ps_y.tile([P, 2, 2, P], F32, name="wt", tag="y")
+                wt = ps_t.tile([P, 2, 2, P], F32, name="wt", tag="pt")
                 for a2 in range(2):
                     for u in range(2):
                         nc.tensor.transpose(
@@ -278,11 +280,14 @@ def tile_informationinteraction_t_kernel(tc, x, conv_w, gamma, beta, out):
             nc.vector.tensor_mul(out=mi[:], in0=mv[:, :, 0], in1=inv[:])
             nc.vector.tensor_sub(out=shift[:], in0=gbt[:, T:2 * T], in1=mi[:])
 
+        y2_banks = [(ps_x, "x"), (ps_y, "y"), (ps_t, "pt"), (ps_t, "pt")]
+
         def pb(u):
             q, a = divmod(u, T)
-            y2 = ps_y.tile([P, 2 * N], F32, name="y2", tag="y")
+            pool, tag = y2_banks[u % 4]
+            y2 = pool.tile([P, 2 * N], F32, name="y2", tag=tag)
             conv(y2[:], q, a)
-            sp = ps_x.tile([P, 2, N], F32, name="sp", tag="x")
+            sp = ps_g.tile([P, 2, N], F32, name="sp", tag="g")
             for j in range(2):
                 b = 2 * q + j
                 nc.tensor.matmul_mx(
@@ -323,36 +328,30 @@ def tile_informationinteraction_t_kernel(tc, x, conv_w, gamma, beta, out):
             if rest == 0 and 0 <= n < count:
                 op(n)
 
-        unit = 0
-        for Q in range(FIRST, LAST):
-            run(tx, B, Q, PREP, 2)
-            run(rc, B, Q, 5, 4)
-            run(qx, PAIRS, Q, PREP + 6, 4)
-            run(bs, UNITS, Q, PREP + 7, 1)
-            run(tg, B, Q, PREP + 2, 2)
-            run(ta, 2 * B, Q, 12, 2)
-            run(gm, 4 * B, Q, 0, 1)
-            run(nrm, B, Q, 6, 4)
-            run(xe, B, Q, PREP, 2)
-            run(mx, 4 * B, Q, 0, 1)
-            run(qa, B, Q, 16, 4)
-            run(ae, 2 * B, Q, 12, 2)
-            if Q == 0:
+        for Q in range(PREP, LAST):
+            run(bs, UNITS, Q, PREP + 11, 2)
+            run(gm1, 4 * B, Q, 0, 1)
+            run(xe, B, Q, PREP + 1, 4)
+            run(nrm, B, Q, 7, 4)
+            run(ta, 2 * B, Q, 9, 2)
+            run(xge, B, Q, PREP + 3, 4)
+            run(tx, B, Q, PREP, 4)
+            run(tg, B, Q, PREP + 2, 4)
+            run(gm2, 4 * B, Q, 0, 1)
+            if Q == 3:
                 prepare_w()
-            if Q == 1:
+            if Q == 4:
                 quantise_w()
                 spread_gamma_beta()
-            if Q == OUT_FIRST - 3:
+            run(qx, PAIRS, Q, PREP + 8, 8)
+            run(ae, 2 * B, Q, 10, 2)
+            run(cv, UNITS, Q, PREP + 10, 2)
+            run(exq, 4 * B, Q, 2, 1)
+            run(rc, B, Q, 5, 4)
+            run(mx, 4 * B, Q, 0, 1)
+            run(qa, B, Q, 12, 4)
+            if Q == LAST - 2:
                 bn_first()
-            if Q == OUT_FIRST - 1:
-                bn_second()
-            while (
-                unit < UNITS
-                and Q >= OUT_FIRST + unit + unit // (OUT_SKIP - 1)
-                and Q > 4 * (2 * (unit // T) + 1) + 16
-            ):
-                pb(unit)
-                unit += 1
-            run(xge, B, Q, PREP + 3, 2)
-            run(cv, UNITS, Q, PREP + 6, 1)
-            run(exq, 4 * B, Q, 1, 1)
+        bn_second()
+        for u in range(UNITS):
+            pb(u)

@@ -21,7 +21,6 @@ EPS = 1e-5
 PAIRS = B // 2
 UNITS = PAIRS * T
 XIN = 8
-XO_BUFS = 12
 FLOPS = 3 * 2 * B * C * C * N
 
 PREP = -3
@@ -31,17 +30,18 @@ LAST = 4 * B + 9
 def tile_informationinteraction_t_kernel(tc, x, conv_w, gamma, beta, out):
     nc = tc.nc
     x_v = x.rearrange("b (s q) h w -> b q s (h w)", q=P)
-    out_v = out.rearrange("b (a m) h w -> a m b (h w)", a=T)
-    w_v = conv_w.rearrange("(a m) c -> m a c", a=T)
+    out_v = out.rearrange("b (m a) h w -> m b (a h w)", a=T)
+    w_v = conv_w.rearrange("(m a) c -> m a c", a=T)
 
     with ExitStack() as ctx:
         keep = ctx.enter_context(tc.tile_pool(name="keep", bufs=1))
-        xin = ctx.enter_context(tc.tile_pool(name="xin", bufs=XO_BUFS))
+        xin = ctx.enter_context(tc.tile_pool(name="xin", bufs=XIN))
         xtp = ctx.enter_context(tc.tile_pool(name="xtp", bufs=4))
         work = ctx.enter_context(tc.tile_pool(name="work", bufs=2))
         epool = ctx.enter_context(tc.tile_pool(name="epool", bufs=12))
         apool = ctx.enter_context(tc.tile_pool(name="apool", bufs=8))
         opool = ctx.enter_context(tc.tile_pool(name="opool", bufs=4))
+        stp = ctx.enter_context(tc.tile_pool(name="stp", bufs=4))
         small = ctx.enter_context(tc.tile_pool(name="small", bufs=4))
         ps_g = ctx.enter_context(tc.psum_pool(name="ps_g", bufs=4))
         ps_x = ctx.enter_context(tc.psum_pool(name="ps_x", bufs=1))
@@ -62,8 +62,10 @@ def tile_informationinteraction_t_kernel(tc, x, conv_w, gamma, beta, out):
         mv = keep.tile([P, T, 2], F32, name="mv")
         inv = keep.tile([P, T], F32, name="inv")
         shift = keep.tile([P, T], F32, name="shift")
-        gb = keep.tile([P, P], BF16, name="gb")
-        gbt = keep.tile([P, 2 * T], F32, name="gbt")
+        gam_b = keep.tile([P, T], BF16, name="gam_b")
+        bet_b = keep.tile([P, T], BF16, name="bet_b")
+        gam = keep.tile([P, T], F32, name="gam")
+        bet = keep.tile([P, T], F32, name="bet")
         ve = keep.tile([P, T], F32, name="ve")
         rsd = keep.tile([P, T], F32, name="rsd")
         mi = keep.tile([P, T], F32, name="mi")
@@ -88,7 +90,7 @@ def tile_informationinteraction_t_kernel(tc, x, conv_w, gamma, beta, out):
         def load_x(b):
             if b >= B:
                 return
-            xn[b] = xin.tile([P, T, N], BF16, name="xn", tag="xo")
+            xn[b] = xin.tile([P, T, N], BF16, name="xn", tag="xn")
             nc.sync.dma_start(out=xn[b][:], in_=x_v[b])
 
         def tx(b):
@@ -157,7 +159,7 @@ def tile_informationinteraction_t_kernel(tc, x, conv_w, gamma, beta, out):
             b, a = divmod(k, T)
             nc.tensor.matmul(
                 out=g_ps[k][:],
-                lhsT=xT[b][:, h, a * P:(a + 1) * P],
+                lhsT=xT[b][:, h].rearrange("n (m a) -> n a m", a=T)[:, a],
                 rhs=xT[b][:, h, :],
                 start=(h == 0),
                 stop=(h == 1),
@@ -264,10 +266,9 @@ def tile_informationinteraction_t_kernel(tc, x, conv_w, gamma, beta, out):
                 in_=w_grp[:].rearrange("p a m t -> p (a m t)"),
             )
 
-        def spread_gamma_beta():
-            gbp = ps_y.tile([P, P], BF16, name="gbp", tag="y")
-            nc.tensor.transpose(out=gbp[:], in_=gb[:], identity=ident[:])
-            nc.vector.tensor_copy(out=gbt[:], in_=gbp[:, 0:2 * T])
+        def cast_gamma_beta():
+            nc.vector.tensor_copy(out=gam[:], in_=gam_b[:])
+            nc.vector.tensor_copy(out=bet[:], in_=bet_b[:])
 
         def bn_first():
             for a in range(T):
@@ -276,10 +277,11 @@ def tile_informationinteraction_t_kernel(tc, x, conv_w, gamma, beta, out):
             nc.gpsimd.tensor_tensor(out=rsd[:], in0=ve[:], in1=mhalf[:], op=ALU.pow)
 
         def bn_second():
-            nc.vector.tensor_mul(out=inv[:], in0=gbt[:, 0:T], in1=rsd[:])
+            nc.vector.tensor_mul(out=inv[:], in0=gam[:], in1=rsd[:])
             nc.vector.tensor_mul(out=mi[:], in0=mv[:, :, 0], in1=inv[:])
-            nc.vector.tensor_sub(out=shift[:], in0=gbt[:, T:2 * T], in1=mi[:])
+            nc.vector.tensor_sub(out=shift[:], in0=bet[:], in1=mi[:])
 
+        o_pair = {}
         y2_banks = [(ps_x, "x"), (ps_y, "y"), (ps_t, "pt"), (ps_t, "pt")]
 
         def pb(u):
@@ -307,9 +309,15 @@ def tile_informationinteraction_t_kernel(tc, x, conv_w, gamma, beta, out):
                 bias=shift[:, a:a + 1],
                 scale=inv[:, a:a + 1],
             )
-            o = xin.tile([P, 2, N], F32, name="o", tag="xo")
-            nc.vector.tensor_tensor(out=o[:], in0=sp[:], in1=r[:], op=ALU.add)
-            nc.sync.dma_start(out=out_v[a, :, 2 * q:2 * q + 2, :], in_=o[:])
+            if a == 0:
+                o_pair[q] = stp.tile([P, 2, T, N], F32, name="o", tag="o")
+            nc.vector.tensor_tensor(out=o_pair[q][:, :, a], in0=sp[:], in1=r[:], op=ALU.add)
+            blocks = 2 if q == PAIRS - 1 else T
+            if (a + 1) % blocks == 0:
+                nc.sync.dma_start(
+                    out=out_v[:, 2 * q:2 * q + 2, (a + 1 - blocks) * N:(a + 1) * N],
+                    in_=o_pair[q][:, :, a + 1 - blocks:a + 1].rearrange("p j a n -> p j (a n)"),
+                )
 
         load_x(0)
         load_x(1)
@@ -319,9 +327,8 @@ def tile_informationinteraction_t_kernel(tc, x, conv_w, gamma, beta, out):
         make_identity(nc, ident[:])
         make_identity(nc, ident32[:])
         nc.gpsimd.memset(mhalf[:], -0.5)
-        nc.vector.memset(gb[:], 0.0)
-        nc.scalar.dma_start(out=gb[0:T, :], in_=gamma.rearrange("(a m) -> a m", a=T))
-        nc.scalar.dma_start(out=gb[T:2 * T, :], in_=beta.rearrange("(a m) -> a m", a=T))
+        nc.scalar.dma_start(out=gam_b[:], in_=gamma.rearrange("(m a) -> m a", a=T))
+        nc.scalar.dma_start(out=bet_b[:], in_=beta.rearrange("(m a) -> m a", a=T))
 
         def run(op, count, quarter, lag, period):
             n, rest = divmod(quarter - lag, period)
@@ -342,7 +349,7 @@ def tile_informationinteraction_t_kernel(tc, x, conv_w, gamma, beta, out):
                 prepare_w()
             if Q == 4:
                 quantise_w()
-                spread_gamma_beta()
+                cast_gamma_beta()
             run(qx, PAIRS, Q, PREP + 8, 8)
             run(ae, 2 * B, Q, 10, 2)
             run(cv, UNITS, Q, PREP + 10, 2)

@@ -24,6 +24,7 @@ XIN = 8
 FLOPS = 3 * 2 * B * C * C * N
 
 PREP = -3
+WARM = 4
 LAST = 4 * B + 9
 
 
@@ -149,7 +150,8 @@ def tile_informationinteraction_t_kernel(tc, x, conv_w, gamma, beta, out):
             )
 
         def cv(u):
-            y_ps[u] = ps_y.tile([P, 2 * N], F32, name="y_ps", tag="y")
+            pool, tag = (ps_x, "x") if u >= UNITS - T and u % 2 == 1 else (ps_y, "y")
+            y_ps[u] = pool.tile([P, 2 * N], F32, name="y_ps", tag=tag)
             conv(y_ps[u][:], u // T, u % T)
 
         def bs(u):
@@ -201,7 +203,8 @@ def tile_informationinteraction_t_kernel(tc, x, conv_w, gamma, beta, out):
         def nrm(b):
             for a in range(T):
                 att[b, a] = apool.tile([P, C], BF16, name="att", tag="att")
-                nc.gpsimd.tensor_scalar(
+                engine = nc.vector if b == B - 1 and a >= 2 else nc.gpsimd
+                engine.tensor_scalar(
                     out=att[b, a][:],
                     in0=ex[b * T + a][:],
                     scalar1=rs[b][:, a:a + 1],
@@ -274,6 +277,8 @@ def tile_informationinteraction_t_kernel(tc, x, conv_w, gamma, beta, out):
             for a in range(T):
                 nc.vector.bn_aggr(out=mv[:, a, :], in_=st[:, a].rearrange("p q s -> p (q s)"))
             nc.vector.tensor_scalar_add(out=ve[:], in0=mv[:, :, 1], scalar1=EPS)
+
+        def bn_pow():
             nc.gpsimd.tensor_tensor(out=rsd[:], in0=ve[:], in1=mhalf[:], op=ALU.pow)
 
         def bn_second():
@@ -330,13 +335,24 @@ def tile_informationinteraction_t_kernel(tc, x, conv_w, gamma, beta, out):
         nc.scalar.dma_start(out=gam_b[:], in_=gamma.rearrange("(m a) -> m a", a=T))
         nc.scalar.dma_start(out=bet_b[:], in_=beta.rearrange("(m a) -> m a", a=T))
 
+        warm = keep.tile([P, C], BF16, name="warm")
+        nc.vector.memset(warm[:], 0.0)
+        warm_ps = ps_y.tile([P, C], F32, name="warm_ps", tag="y")
+        for n in range(WARM):
+            nc.tensor.matmul(
+                out=warm_ps[:], lhsT=warm[:, 0:P], rhs=warm[:], start=True, stop=True
+            )
+
         def run(op, count, quarter, lag, period):
             n, rest = divmod(quarter - lag, period)
             if rest == 0 and 0 <= n < count:
                 op(n)
 
         for Q in range(PREP, LAST):
-            run(bs, UNITS, Q, PREP + 11, 2)
+            run(bs, UNITS - T, Q, PREP + 11, 2)
+            if Q == 4 * B:
+                bs(UNITS - 4)
+                bs(UNITS - 3)
             run(gm1, 4 * B, Q, 0, 1)
             run(xe, B, Q, PREP + 1, 4)
             run(nrm, B, Q, 7, 4)
@@ -352,13 +368,24 @@ def tile_informationinteraction_t_kernel(tc, x, conv_w, gamma, beta, out):
                 cast_gamma_beta()
             run(qx, PAIRS, Q, PREP + 8, 8)
             run(ae, 2 * B, Q, 10, 2)
-            run(cv, UNITS, Q, PREP + 10, 2)
+            run(cv, UNITS - T, Q, PREP + 10, 2)
+            if Q == 4 * B - 1:
+                cv(UNITS - 4)
+                cv(UNITS - 3)
+            if Q == 4 * B:
+                cv(UNITS - 2)
+                cv(UNITS - 1)
             run(exq, 4 * B, Q, 2, 1)
             run(rc, B, Q, 5, 4)
             run(mx, 4 * B, Q, 0, 1)
             run(qa, B, Q, 12, 4)
-            if Q == LAST - 2:
+            if Q == 4 * B + 1:
+                bs(UNITS - 2)
+                bs(UNITS - 1)
                 bn_first()
-        bn_second()
+            if Q == 4 * B + 3:
+                bn_pow()
+            if Q == 4 * B + 5:
+                bn_second()
         for u in range(UNITS):
             pb(u)

from contextlib import ExitStack

import concourse.mybir as mybir
from concourse.masks import make_identity

F32 = mybir.dt.float32
BF16 = mybir.dt.bfloat16
U32 = mybir.dt.uint32
U8 = mybir.dt.uint8
FP8X4 = mybir.dt.float8_e4m3fn_x4
ACT = mybir.ActivationFunctionType
ALU = mybir.AluOpType
AX = mybir.AxisListType

B = 28
C = 512
N = 256
P = 128
T = 4
EPS = 1e-5
PAIRS = B // 2
UNITS = PAIRS * T
XIN = 8
FLOPS = 3 * 2 * B * C * C * N

PREP = -3
WARM = 4
LAST = 4 * B + 9


def tile_informationinteraction_t_kernel(tc, x, conv_w, gamma, beta, out):
    nc = tc.nc
    x_v = x.rearrange("b (s q) h w -> b q s (h w)", q=P)
    out_v = out.rearrange("b (m a) h w -> m b (a h w)", a=T)
    w_v = conv_w.rearrange("(m a) c -> m a c", a=T)

    with ExitStack() as ctx:
        keep = ctx.enter_context(tc.tile_pool(name="keep", bufs=1))
        xin = ctx.enter_context(tc.tile_pool(name="xin", bufs=XIN))
        xtp = ctx.enter_context(tc.tile_pool(name="xtp", bufs=4))
        work = ctx.enter_context(tc.tile_pool(name="work", bufs=2))
        epool = ctx.enter_context(tc.tile_pool(name="epool", bufs=12))
        apool = ctx.enter_context(tc.tile_pool(name="apool", bufs=8))
        opool = ctx.enter_context(tc.tile_pool(name="opool", bufs=4))
        stp = ctx.enter_context(tc.tile_pool(name="stp", bufs=4))
        small = ctx.enter_context(tc.tile_pool(name="small", bufs=4))
        ps_g = ctx.enter_context(tc.psum_pool(name="ps_g", bufs=4))
        ps_x = ctx.enter_context(tc.psum_pool(name="ps_x", bufs=1))
        ps_y = ctx.enter_context(tc.psum_pool(name="ps_y", bufs=1))
        ps_t = ctx.enter_context(tc.psum_pool(name="ps_t", bufs=2))
        ctx.enter_context(tc.manual_schedule())

        ident = keep.tile([P, P], BF16, name="ident")
        ident32 = keep.tile([P, P], F32, name="ident32")
        mhalf = keep.tile([P, T], F32, name="mhalf")
        xq = keep.tile([P, B * N], U32, name="xq", align_bytes=64)
        xs = keep.tile([P, B * N], U8, name="xs", align_bytes=64)
        aq = keep.tile([P, B * C], U32, name="aq", align_bytes=64)
        asc = keep.tile([P, B * C], U8, name="asc", align_bytes=64)
        wq = keep.tile([P, C], U32, name="wq", align_bytes=64)
        ws = keep.tile([P, C], U8, name="ws", align_bytes=64)
        st = keep.tile([P, T, PAIRS, 6], F32, name="st")
        mv = keep.tile([P, T, 2], F32, name="mv")
        inv = keep.tile([P, T], F32, name="inv")
        shift = keep.tile([P, T], F32, name="shift")
        gam_b = keep.tile([P, T], BF16, name="gam_b")
        bet_b = keep.tile([P, T], BF16, name="bet_b")
        gam = keep.tile([P, T], F32, name="gam")
        bet = keep.tile([P, T], F32, name="bet")
        ve = keep.tile([P, T], F32, name="ve")
        rsd = keep.tile([P, T], F32, name="rsd")
        mi = keep.tile([P, T], F32, name="mi")
        w_sb = keep.tile([P, T, C], BF16, name="w_sb")
        w_grp = keep.tile([P, T, P, T], BF16, name="w_grp", align_bytes=64)

        xn = {}
        xt_ps = {}
        xT = {}
        xg_ps = {}
        xg = {}
        y_ps = {}
        g_ps = {}
        nm = {}
        ssum = {}
        rs = {}
        ex = {}
        att = {}
        pt = {}
        ag = {}

        def load_x(b):
            if b >= B:
                return
            xn[b] = xin.tile([P, T, N], BF16, name="xn", tag="xn")
            nc.sync.dma_start(out=xn[b][:], in_=x_v[b])

        def tx(b):
            xt_ps[b] = ps_x.tile([P, 2, C], BF16, name="xt_ps", tag="x")
            for h in range(2):
                for s in range(T):
                    nc.tensor.transpose(
                        out=xt_ps[b][:, h, s * P:(s + 1) * P],
                        in_=xn[b][:, s, h * P:(h + 1) * P],
                        identity=ident[:],
                    )
            load_x(b + XIN)

        def xe(b):
            xT[b] = xtp.tile([P, 2, C], BF16, name="xT", tag="xT")
            nc.scalar.copy(out=xT[b][:].bitcast(F32), in_=xt_ps[b][:].bitcast(F32))

        def tg(b):
            xg_ps[b] = ps_x.tile([P, 2, 2, P], F32, name="xg_ps", tag="x")
            words = xT[b][:].bitcast(F32)
            for h in range(2):
                for u in range(2):
                    nc.tensor.transpose(
                        out=xg_ps[b][:, h, u, :],
                        in_=words[:, h, u * P:(u + 1) * P],
                        identity=ident32[:],
                    )

        def xge(b):
            if b % 2 == 0:
                xg[b // 2] = work.tile([P, 2, N, T], BF16, name="xg", tag="xg", align_bytes=64)
            words = xg[b // 2][:, b % 2].rearrange("p n t -> p (n t)").bitcast(F32)
            nc.scalar.copy(
                out=words.rearrange("p (h n u) -> p h n u", h=2, u=2),
                in_=xg_ps[b][:].rearrange("p h u n -> p h n u"),
            )

        def qx(q):
            cols = slice(q * 2 * N, (q + 1) * 2 * N)
            nc.vector.quantize_mx(
                out=xq[:, cols].bitcast(FP8X4),
                scales=xs[:, cols],
                in_=xg[q][:].rearrange("p j n t -> p (j n t)"),
            )

        def conv(dst, q, a):
            cols = slice(q * 2 * N, (q + 1) * 2 * N)
            nc.tensor.matmul_mx(
                out=dst,
                lhsT=wq[:, a * P:(a + 1) * P].bitcast(FP8X4),
                lhsT_scale=ws[:, a * P:(a + 1) * P],
                rhs=xq[:, cols].bitcast(FP8X4),
                rhs_scale=xs[:, cols],
                start=True,
                stop=True,
            )

        def cv(u):
            pool, tag = (ps_x, "x") if u >= UNITS - T and u % 2 == 1 else (ps_y, "y")
            y_ps[u] = pool.tile([P, 2 * N], F32, name="y_ps", tag=tag)
            conv(y_ps[u][:], u // T, u % T)

        def bs(u):
            nc.vector.bn_stats(out=st[:, u % T, u // T, :], in_=y_ps[u][:])

        def gram_half(k, h):
            b, a = divmod(k, T)
            nc.tensor.matmul(
                out=g_ps[k][:],
                lhsT=xT[b][:, h].rearrange("n (m a) -> n a m", a=T)[:, a],
                rhs=xT[b][:, h, :],
                start=(h == 0),
                stop=(h == 1),
            )

        def gm1(k):
            g_ps[k] = ps_g.tile([P, C], F32, name="g_ps", tag="g")
            gram_half(k, 0)

        def gm2(k):
            gram_half(k, 1)

        def mx(k):
            b, a = divmod(k, T)
            if a == 0:
                nm[b] = small.tile([P, T], F32, name="nm", tag="nm")
            nc.vector.tensor_reduce(
                out=nm[b][:, a:a + 1], in_=g_ps[k][:], axis=AX.X, op=ALU.max, negate=True
            )

        def exq(k):
            b, a = divmod(k, T)
            if a == 0:
                ssum[b] = small.tile([P, T], F32, name="ssum", tag="ssum")
            ex[k] = epool.tile([P, C], F32, name="ex", tag="e")
            nc.scalar.activation(
                out=ex[k][:],
                in_=g_ps[k][:],
                func=ACT.Exp,
                bias=nm[b][:, a:a + 1],
                scale=1.0,
                accum_out=ssum[b][:, a:a + 1],
            )

        def rc(b):
            rs[b] = small.tile([P, T], F32, name="rs", tag="rs")
            nc.vector.reciprocal(out=rs[b][:], in_=ssum[b][:])

        def nrm(b):
            for a in range(T):
                att[b, a] = apool.tile([P, C], BF16, name="att", tag="att")
                engine = nc.vector if b == B - 1 and a >= 2 else nc.gpsimd
                engine.tensor_scalar(
                    out=att[b, a][:],
                    in0=ex[b * T + a][:],
                    scalar1=rs[b][:, a:a + 1],
                    scalar2=0.0,
                    op0=ALU.mult,
                    op1=ALU.add,
                )

        def ta(k):
            b, half = divmod(k, 2)
            pt[k] = ps_t.tile([P, 2, 2, P], F32, name="pt", tag="pt")
            for a2 in range(2):
                words = att[b, 2 * half + a2][:].bitcast(F32)
                for u in range(2):
                    nc.tensor.transpose(
                        out=pt[k][:, a2, u, :],
                        in_=words[:, u * P:(u + 1) * P],
                        identity=ident32[:],
                    )

        def ae(k):
            b, half = divmod(k, 2)
            if half == 0:
                ag[b] = work.tile([P, T, P, T], BF16, name="ag", tag="ag", align_bytes=64)
            words = ag[b][:].rearrange("p a m t -> p a (m t)").bitcast(F32).rearrange(
                "p a (m u) -> p a m u", u=2
            )
            nc.scalar.copy(
                out=words[:, 2 * half:2 * half + 2],
                in_=pt[k][:].rearrange("p a u m -> p a m u"),
            )

        def qa(b):
            nc.vector.quantize_mx(
                out=aq[:, b * C:(b + 1) * C].bitcast(FP8X4),
                scales=asc[:, b * C:(b + 1) * C],
                in_=ag[b][:].rearrange("p a m t -> p (a m t)"),
            )

        def prepare_w():
            w32 = w_sb[:].bitcast(F32)
            g32 = w_grp[:].rearrange("p a m t -> p a (m t)").bitcast(F32).rearrange(
                "p a (m u) -> p a m u", u=2
            )
            for k in range(2):
                wt = ps_t.tile([P, 2, 2, P], F32, name="wt", tag="pt")
                for a2 in range(2):
                    for u in range(2):
                        nc.tensor.transpose(
                            out=wt[:, a2, u, :],
                            in_=w32[:, 2 * k + a2, u * P:(u + 1) * P],
                            identity=ident32[:],
                        )
                nc.scalar.copy(
                    out=g32[:, 2 * k:2 * k + 2], in_=wt[:].rearrange("p a u m -> p a m u")
                )

        def quantise_w():
            nc.vector.quantize_mx(
                out=wq[:].bitcast(FP8X4),
                scales=ws[:],
                in_=w_grp[:].rearrange("p a m t -> p (a m t)"),
            )

        def cast_gamma_beta():
            nc.vector.tensor_copy(out=gam[:], in_=gam_b[:])
            nc.vector.tensor_copy(out=bet[:], in_=bet_b[:])

        def bn_first():
            for a in range(T):
                nc.vector.bn_aggr(out=mv[:, a, :], in_=st[:, a].rearrange("p q s -> p (q s)"))
            nc.vector.tensor_scalar_add(out=ve[:], in0=mv[:, :, 1], scalar1=EPS)

        def bn_pow():
            nc.gpsimd.tensor_tensor(out=rsd[:], in0=ve[:], in1=mhalf[:], op=ALU.pow)

        def bn_second():
            nc.vector.tensor_mul(out=inv[:], in0=gam[:], in1=rsd[:])
            nc.vector.tensor_mul(out=mi[:], in0=mv[:, :, 0], in1=inv[:])
            nc.vector.tensor_sub(out=shift[:], in0=bet[:], in1=mi[:])

        o_pair = {}
        y2_banks = [(ps_x, "x"), (ps_y, "y"), (ps_t, "pt"), (ps_t, "pt")]

        def pb(u):
            q, a = divmod(u, T)
            pool, tag = y2_banks[u % 4]
            y2 = pool.tile([P, 2 * N], F32, name="y2", tag=tag)
            conv(y2[:], q, a)
            sp = ps_g.tile([P, 2, N], F32, name="sp", tag="g")
            for j in range(2):
                b = 2 * q + j
                nc.tensor.matmul_mx(
                    out=sp[:, j, :],
                    lhsT=aq[:, b * C + a * P:b * C + (a + 1) * P].bitcast(FP8X4),
                    lhsT_scale=asc[:, b * C + a * P:b * C + (a + 1) * P],
                    rhs=xq[:, b * N:(b + 1) * N].bitcast(FP8X4),
                    rhs_scale=xs[:, b * N:(b + 1) * N],
                    start=True,
                    stop=True,
                )
            r = opool.tile([P, 2, N], F32, name="r", tag="r")
            nc.scalar.activation(
                out=r[:].rearrange("p j n -> p (j n)"),
                in_=y2[:],
                func=ACT.Relu,
                bias=shift[:, a:a + 1],
                scale=inv[:, a:a + 1],
            )
            if a == 0:
                o_pair[q] = stp.tile([P, 2, T, N], F32, name="o", tag="o")
            nc.vector.tensor_tensor(out=o_pair[q][:, :, a], in0=sp[:], in1=r[:], op=ALU.add)
            blocks = 2 if q == PAIRS - 1 else T
            if (a + 1) % blocks == 0:
                nc.sync.dma_start(
                    out=out_v[:, 2 * q:2 * q + 2, (a + 1 - blocks) * N:(a + 1) * N],
                    in_=o_pair[q][:, :, a + 1 - blocks:a + 1].rearrange("p j a n -> p j (a n)"),
                )

        load_x(0)
        load_x(1)
        nc.sync.dma_start(out=w_sb[:], in_=w_v)
        for b in range(2, XIN):
            load_x(b)
        make_identity(nc, ident[:])
        make_identity(nc, ident32[:])
        nc.gpsimd.memset(mhalf[:], -0.5)
        nc.scalar.dma_start(out=gam_b[:], in_=gamma.rearrange("(m a) -> m a", a=T))
        nc.scalar.dma_start(out=bet_b[:], in_=beta.rearrange("(m a) -> m a", a=T))

        warm = keep.tile([P, C], BF16, name="warm")
        nc.vector.memset(warm[:], 0.0)
        warm_ps = ps_y.tile([P, C], F32, name="warm_ps", tag="y")
        for n in range(WARM):
            nc.tensor.matmul(
                out=warm_ps[:], lhsT=warm[:, 0:P], rhs=warm[:], start=True, stop=True
            )

        def run(op, count, quarter, lag, period):
            n, rest = divmod(quarter - lag, period)
            if rest == 0 and 0 <= n < count:
                op(n)

        for Q in range(PREP, LAST):
            run(bs, UNITS - T, Q, PREP + 11, 2)
            if Q == 4 * B:
                bs(UNITS - 4)
                bs(UNITS - 3)
            run(gm1, 4 * B, Q, 0, 1)
            run(xe, B, Q, PREP + 1, 4)
            run(nrm, B, Q, 7, 4)
            run(ta, 2 * B, Q, 9, 2)
            run(xge, B, Q, PREP + 3, 4)
            run(tx, B, Q, PREP, 4)
            run(tg, B, Q, PREP + 2, 4)
            run(gm2, 4 * B, Q, 0, 1)
            if Q == 3:
                prepare_w()
            if Q == 4:
                quantise_w()
                cast_gamma_beta()
            run(qx, PAIRS, Q, PREP + 8, 8)
            run(ae, 2 * B, Q, 10, 2)
            run(cv, UNITS - T, Q, PREP + 10, 2)
            if Q == 4 * B - 1:
                cv(UNITS - 4)
                cv(UNITS - 3)
            if Q == 4 * B:
                cv(UNITS - 2)
                cv(UNITS - 1)
            run(exq, 4 * B, Q, 2, 1)
            run(rc, B, Q, 5, 4)
            run(mx, 4 * B, Q, 0, 1)
            run(qa, B, Q, 12, 4)
            if Q == 4 * B + 1:
                bs(UNITS - 2)
                bs(UNITS - 1)
                bn_first()
            if Q == 4 * B + 3:
                bn_pow()
            if Q == 4 * B + 5:
                bn_second()
        for u in range(UNITS):
            pb(u)
